import numpy as np
import ml_dtypes


def mxq(x, axis, fmt="e4m3"):
    dtype, down = {"e4m3": (ml_dtypes.float8_e4m3fn, 7), "e5m2": (ml_dtypes.float8_e5m2, 14)}[fmt]
    v = np.moveaxis(np.asarray(x, np.float32).astype(ml_dtypes.bfloat16).astype(np.float64), axis, -1)
    blocks = v.reshape(v.shape[:-1] + (-1, 32))
    amax = np.abs(blocks).max(-1, keepdims=True)
    byte = np.maximum(np.where(amax > 0, np.frexp(amax)[1] - 1 + 127, 0) - down, 1)
    scale = np.exp2(byte - 127.0)
    codes = (blocks / scale).astype(np.float32).astype(dtype).astype(np.float64)
    return np.moveaxis((codes * scale).reshape(v.shape), -1, axis)


WIDE = False


def mx_kscale(k):
    if not WIDE:
        return np.ones(k)
    levels = np.array([10, -10, 5, -5, 0])
    a = np.random.permutation(np.resize(levels, k // 512 * 4)).reshape(k // 512, 4)
    idx = np.arange(k)
    return np.exp2(a[idx // 512, idx % 128 // 32])


BF16 = ml_dtypes.bfloat16


def bf(x):
    return np.asarray(x, np.float32).astype(BF16)


def f64(x):
    return np.asarray(x).astype(np.float64)


E2M1 = np.array([0.0, 0.5, 1.0, 1.5, 2.0, 3.0, 4.0, 6.0, -0.0, -0.5, -1.0, -1.5, -2.0, -3.0, -4.0, -6.0])


def pack_weight(w, fmt):
    k, n = w.shape
    w = f64(bf(w)).reshape(k // 32, 32, n)
    amax = np.abs(w).max(1)
    if fmt == "e4m3":
        byte = np.frexp(amax)[1] - 1 + 127 - 7
    else:
        mant, ex = np.frexp(amax / 6.0)
        byte = np.where(mant > 0.5, ex, ex - 1) + 127
    byte = np.clip(np.where(amax > 0, byte, 1), 1, 254)
    scaled = (w * np.exp2(127.0 - byte)[:, None, :]).reshape(k, n).astype(np.float32)
    by_word = np.ascontiguousarray(scaled.reshape(k // 512, 128, 4, n).transpose(0, 1, 3, 2))
    if fmt == "e4m3":
        words = by_word.astype(ml_dtypes.float8_e4m3fn).view(np.uint8)
    else:
        c = by_word.astype(ml_dtypes.float4_e2m1fn).view(np.uint8) & 0xF
        words = c[..., 0::2] | (c[..., 1::2] << 4)
    return np.ascontiguousarray(words), np.ascontiguousarray(byte.astype(np.uint8).reshape(k // 512, 16, n))


def unpack_weight(words, scales, fmt):
    g, p, n, _ = words.shape
    if fmt == "e4m3":
        vals = np.ascontiguousarray(words).view(ml_dtypes.float8_e4m3fn).astype(np.float64)
    else:
        nib = np.empty((g, p, n, 4), np.uint8)
        nib[..., 0::2] = words & 0xF
        nib[..., 1::2] = words >> 4
        vals = E2M1[nib]
    vals = vals * np.repeat(np.exp2(scales.astype(np.float64) - 127.0), 8, axis=1)[..., None]
    return vals.transpose(0, 1, 3, 2).reshape(g * 512, n)


B, C, H, W, L = 1, 512, 32, 32, 6
N = H * W
EPS = 1e-5
QS = (24.0 / C) ** 0.25
VS = 0.75
FMT = "e4m3"


def relu_draw():
    return np.maximum(np.random.standard_normal((B, C, H, W)), 0.0)


def setup_inputs():
    t = mx_kscale(C)
    q = bf(relu_draw() * QS)
    k = bf(relu_draw() * QS)
    v = bf(relu_draw() * VS * t[None, :, None, None])
    w_up = np.random.standard_normal((C, C)) * 2.0 / np.sqrt(C) / t[None, :]
    words, scales = pack_weight(np.ascontiguousarray(w_up.T), FMT)
    return {"q": q,
            "k": k,
            "v": v,
            "w_up_words": words,
            "w_up_scales": scales,
            "gamma": bf(np.random.uniform(size=C)),
            "beta": bf(np.random.standard_normal(C) * 0.1),
            "mean": bf(np.random.standard_normal(C) * 0.1),
            "var": bf(np.random.uniform(size=C) + 0.5)}


def reference(q, k, v, w_up_words, w_up_scales, gamma, beta, mean, var):
    qm = f64(q).reshape(B, C, N).transpose(0, 2, 1)
    km = f64(k).reshape(B, C, N)
    vm = f64(v).reshape(B, C, N).transpose(0, 2, 1)
    sim = qm @ km
    e = np.exp(sim - sim.max(-1, keepdims=True))
    ctx = (mxq(e, 2, "e4m3") @ mxq(vm, 1, "e4m3")) / e.sum(-1, keepdims=True)
    ctx_t = ctx.transpose(0, 2, 1)
    y = unpack_weight(w_up_words, w_up_scales, FMT).T @ mxq(ctx_t, 1, "e4m3")
    a = (f64(gamma) / np.sqrt(f64(var) + EPS))[:, None]
    out = np.maximum((y - f64(mean)[:, None]) * a + f64(beta)[:, None], 0.0)
    return out.reshape(B, C, H, W)

@@ -1,0 +1,357 @@
+from contextlib import ExitStack
+
+import concourse.mybir as mybir
+from concourse.masks import make_identity
+
+F32 = mybir.dt.float32
+BF16 = mybir.dt.bfloat16
+I32 = mybir.dt.int32
+U32 = mybir.dt.uint32
+U8 = mybir.dt.uint8
+FP8X4 = mybir.dt.float8_e4m3fn_x4
+ACT = mybir.ActivationFunctionType
+ALU = mybir.AluOpType
+AXIS = mybir.AxisListType
+
+P = 128
+PACK = 4
+CHANNELS = 512
+PIXELS = 1024
+EPS = 1e-5
+C_CHUNKS = CHANNELS // P
+HALF = 512
+N_TILES = PIXELS // P
+K_PASSES = PIXELS // (P * PACK)
+GROUP = 2
+GROUP_COLS = GROUP * P
+N_GROUPS = N_TILES // GROUP
+E_LAG = 2
+BN_STEP = 1
+V_STEP = 2
+RB_STEP = 6
+LAST_E_ROUND = 3
+W_LAG = 4
+
+FLOPS = 2 * PIXELS * PIXELS * CHANNELS * 2 + 2 * CHANNELS * CHANNELS * PIXELS
+
+
+def tile_objectattention_pa_kernel(
+    tc, q, k, v, w_up_words, w_up_scales, gamma, beta, mean, var, out
+):
+    nc = tc.nc
+    q_view = q[0].rearrange("(j p) h w -> p j (h w)", p=P)
+    k_view = k[0].rearrange("(j p) h w -> p j (h w)", p=P)
+    v_view = v[0].rearrange("(p t) h w -> p t (h w)", t=PACK)
+    out_view = out[0].rearrange("(j p) h w -> p j (h w)", p=P)
+
+    with ExitStack() as ctx:
+        keep = ctx.enter_context(tc.tile_pool(name="keep", bufs=1))
+        ring = ctx.enter_context(tc.tile_pool(name="ring", bufs=3))
+        y_pool = ctx.enter_context(tc.tile_pool(name="y_pool", bufs=N_GROUPS))
+        acc_ps = ctx.enter_context(tc.psum_pool(name="acc_ps", bufs=4))
+        et_ps = ctx.enter_context(tc.psum_pool(name="et_ps", bufs=2))
+        aux_ps = ctx.enter_context(tc.psum_pool(name="aux_ps", bufs=2))
+        ctx.enter_context(tc.manual_schedule())
+
+        q_sb = keep.tile([P, C_CHUNKS, PIXELS], BF16)
+        k_sb = keep.tile([P, C_CHUNKS, PIXELS], BF16)
+        v_sb = keep.tile([P, PACK, PIXELS], BF16)
+        ident_f32 = keep.tile([P, P], F32)
+        ident_bf16 = keep.tile([P, P], BF16)
+        bn_rows = keep.tile([P, P], BF16)
+        bn_cols = keep.tile([P, 4 * C_CHUNKS], F32)
+        minus_half = keep.tile([P, C_CHUNKS], F32)
+        bn_var_eps = keep.tile([P, C_CHUNKS], F32)
+        bn_rstd = keep.tile([P, C_CHUNKS], F32)
+        bn_scale = keep.tile([P, C_CHUNKS], F32)
+        bn_shift = keep.tile([P, C_CHUNKS], F32)
+        bn_bias = keep.tile([P, C_CHUNKS], F32)
+        table_in = keep.tile([P, 1], F32)
+        table_out = keep.tile([P, 1], F32)
+        half_max = keep.tile([P, N_TILES, 2], F32)
+        neg_max = keep.tile([P, N_TILES], F32)
+        half_sum = keep.tile([P, N_TILES, 2], F32)
+        row_sum = keep.tile([P, N_TILES], F32)
+        row_inv = keep.tile([P, N_TILES], F32)
+        inv_spread = keep.tile([P, PIXELS], F32)
+        w_codes = keep.tile([P, CHANNELS], U32, align_bytes=64)
+        w_plane = keep.tile([P, CHANNELS], U8, align_bytes=64)
+        v_grouped = keep.tile([P, K_PASSES, CHANNELS, PACK], BF16, align_bytes=64)
+        v_codes = keep.tile([P, K_PASSES, CHANNELS], U32, align_bytes=64)
+        v_plane = keep.tile([P, K_PASSES, CHANNELS], U8, align_bytes=64)
+        e_codes = keep.tile([P, N_TILES, K_PASSES, P], U32, align_bytes=64)
+        e_plane = keep.tile([P, N_TILES, K_PASSES, P], U8, align_bytes=64)
+        c_codes = keep.tile([P, PIXELS], U32, align_bytes=64)
+        c_plane = keep.tile([P, PIXELS], U8, align_bytes=64)
+
+        nc.vector.memset(table_in[:], 0.0)
+        nc.vector.memset(bn_rows[:], 0.0)
+        nc.vector.memset(w_plane[:].bitcast(I32), 0)
+        nc.scalar.activation(out=table_out[:], in_=table_in[:], func=ACT.Exp)
+        make_identity(nc, ident_bf16[:])
+        make_identity(nc, ident_f32[:])
+        nc.gpsimd.memset(minus_half[:], -0.5)
+
+        first_q = GROUP_COLS
+        for j in range(C_CHUNKS):
+            nc.sync.dma_start(out=q_sb[:, j, 0:first_q], in_=q_view[:, j, 0:first_q])
+            nc.sync.dma_start(out=k_sb[:, j, 0:HALF], in_=k_view[:, j, 0:HALF])
+        for j in range(C_CHUNKS):
+            nc.sync.dma_start(out=k_sb[:, j, HALF:PIXELS], in_=k_view[:, j, HALF:PIXELS])
+        for row, vector in enumerate((gamma, beta, mean, var)):
+            nc.sync.dma_start(
+                out=bn_rows[C_CHUNKS * row : C_CHUNKS * (row + 1), :],
+                in_=vector.rearrange("(j p) -> j p", p=P),
+            )
+        nc.sync.dma_start(out=q_sb[:, :, first_q:HALF], in_=q_view[:, :, first_q:HALF])
+        for g in range(K_PASSES):
+            keys = slice(g * HALF, (g + 1) * HALF)
+            nc.sync.dma_start(out=v_sb[:, :, keys], in_=v_view[:, :, keys])
+        nc.sync.dma_start(out=q_sb[:, :, HALF:PIXELS], in_=q_view[:, :, HALF:PIXELS])
+        nc.sync.dma_start(
+            out=w_codes[:].bitcast(I32),
+            in_=w_up_words[0].rearrange("p n t -> p (n t)").bitcast(I32),
+        )
+        for quad in range(4):
+            nc.sync.dma_start(
+                out=w_plane[32 * quad : 32 * quad + 4, :].bitcast(I32),
+                in_=w_up_scales[0, 4 * quad : 4 * quad + 4, :].bitcast(I32),
+            )
+
+        s_bank = {}
+        e_sb = {}
+        e_t = {}
+        e_grouped = {}
+        v_t = {}
+        inv_t = {}
+        ctx_ps = {}
+        ctx_grouped = {}
+        v_words = v_sb[:].bitcast(F32)
+
+        def transpose_e(i, c):
+            if c == 0:
+                e_t[i] = et_ps.tile([P, 2 * K_PASSES, P], F32, name="e_t", tag="e_t")
+            nc.tensor.transpose(
+                e_t[i][:, c, :], e_sb[i][:].bitcast(F32)[:, c * P : (c + 1) * P], ident_f32[:]
+            )
+
+        def evacuate_e(i):
+            e_grouped[i] = ring.tile(
+                [P, K_PASSES, P, PACK], BF16, name="e_grouped", tag="e_grouped", align_bytes=64
+            )
+            nc.scalar.copy(
+                out=e_grouped[i][:].bitcast(F32),
+                in_=e_t[i][:].rearrange("p (g u) n -> p g n u", u=2),
+            )
+
+        def quantise_e(i):
+            nc.vector.quantize_mx(
+                out=e_codes[:, i].rearrange("p g n -> p (g n)").bitcast(FP8X4),
+                scales=e_plane[:, i].rearrange("p g n -> p (g n)"),
+                in_=e_grouped[i][:].rearrange("p g n t -> p (g n t)"),
+            )
+
+        def transpose_v(bank, r):
+            g, pair = divmod(bank, 2)
+            u, second = divmod(r, 2)
+            t = 2 * pair + second
+            if r == 0:
+                v_t[bank] = aux_ps.tile([P, 2, 2 * P], F32, name="v_t", tag="aux")
+            first_word = (2 * g + u) * P
+            nc.tensor.transpose(
+                v_t[bank][:, u, second * P : (second + 1) * P],
+                v_words[:, t, first_word : first_word + P],
+                ident_f32[:],
+            )
+
+        def evacuate_v(bank):
+            g, pair = divmod(bank, 2)
+            columns = slice(pair * 2 * P, (pair + 1) * 2 * P)
+            nc.vector.tensor_copy(
+                out=v_grouped[:, g, columns, :].bitcast(F32),
+                in_=v_t[bank][:].rearrange("p u c -> p c u"),
+            )
+
+        def quantise_v(g):
+            nc.vector.quantize_mx(
+                out=v_codes[:, g, :].bitcast(FP8X4),
+                scales=v_plane[:, g, :],
+                in_=v_grouped[:, g].rearrange("p c t -> p (c t)"),
+            )
+
+        def invert_row_sums(half):
+            tiles = slice(half * 4, (half + 1) * 4)
+            nc.vector.tensor_reduce(
+                out=row_sum[:, tiles], in_=half_sum[:, tiles, :], axis=AXIS.X, op=ALU.add
+            )
+            nc.vector.reciprocal(out=row_inv[:, tiles], in_=row_sum[:, tiles])
+
+        def spread_inverse(half, r):
+            if r == 0:
+                inv_t[half] = aux_ps.tile([P, 4, P], F32, name="inv_t", tag="aux")
+            i = half * 4 + r
+            nc.tensor.transpose(
+                inv_t[half][:, r, :], row_inv[:, i : i + 1].to_broadcast([P, P]), ident_f32[:]
+            )
+
+        def evacuate_inverse(half):
+            nc.scalar.copy(
+                out=inv_spread[:, half * HALF : (half + 1) * HALF],
+                in_=inv_t[half][:].rearrange("p r n -> p (r n)"),
+            )
+
+        def attend(i):
+            ctx_ps[i] = aux_ps.tile([P, PACK, P], F32, name="ctx_ps", tag="aux")
+            for t in range(PACK):
+                for g in range(K_PASSES):
+                    nc.tensor.matmul_mx(
+                        out=ctx_ps[i][:, t, :],
+                        lhsT=v_codes[:, g, t * P : (t + 1) * P].bitcast(FP8X4),
+                        lhsT_scale=v_plane[:, g, t * P : (t + 1) * P],
+                        rhs=e_codes[:, i, g, :].bitcast(FP8X4),
+                        rhs_scale=e_plane[:, i, g, :],
+                        start=(g == 0),
+                        stop=(g == K_PASSES - 1),
+                    )
+
+        def normalise(i):
+            ctx_grouped[i] = ring.tile(
+                [P, P, PACK], BF16, name="ctx_grouped", tag="ctx_grouped", align_bytes=64
+            )
+            nc.vector.tensor_tensor(
+                out=ctx_grouped[i][:],
+                in0=ctx_ps[i][:].rearrange("p t n -> p n t"),
+                in1=inv_spread[:, i * P : (i + 1) * P].unsqueeze(2).to_broadcast([P, P, PACK]),
+                op=ALU.mult,
+            )
+
+        def quantise_ctx(i):
+            nc.vector.quantize_mx(
+                out=c_codes[:, i * P : (i + 1) * P].bitcast(FP8X4),
+                scales=c_plane[:, i * P : (i + 1) * P],
+                in_=ctx_grouped[i][:].rearrange("p n t -> p (n t)"),
+            )
+
+        def project(group):
+            queries = slice(group * GROUP_COLS, (group + 1) * GROUP_COLS)
+            y_sb = y_pool.tile([P, C_CHUNKS, GROUP_COLS], F32, name="y_sb", tag="y_sb")
+            for pair in range(C_CHUNKS // 2):
+                y_bank = acc_ps.tile([P, 2, GROUP_COLS], F32, name="y_bank", tag="acc")
+                for second in range(2):
+                    j = 2 * pair + second
+                    nc.tensor.matmul_mx(
+                        out=y_bank[:, second, :],
+                        lhsT=w_codes[:, j * P : (j + 1) * P].bitcast(FP8X4),
+                        lhsT_scale=w_plane[:, j * P : (j + 1) * P],
+                        rhs=c_codes[:, queries].bitcast(FP8X4),
+                        rhs_scale=c_plane[:, queries],
+                        start=True,
+                        stop=True,
+                    )
+                for second in range(2):
+                    j = 2 * pair + second
+                    nc.scalar.activation(
+                        out=y_sb[:, j, :],
+                        in_=y_bank[:, second, :],
+                        func=ACT.Relu,
+                        bias=bn_bias[:, j : j + 1],
+                        scale=bn_scale[:, j : j + 1],
+                    )
+            nc.sync.dma_start(out=out_view[:, :, queries], in_=y_sb[:])
+
+        for i in range(N_TILES):
+            for h in range(2):
+                s_bank[(i, h)] = acc_ps.tile([P, HALF], F32, name="s_bank", tag="acc")
+                for j in range(C_CHUNKS):
+                    nc.tensor.matmul(
+                        out=s_bank[(i, h)][:],
+                        lhsT=q_sb[:, j, i * P : (i + 1) * P],
+                        rhs=k_sb[:, j, h * HALF : (h + 1) * HALF],
+                        start=(j == 0),
+                        stop=(j == C_CHUNKS - 1),
+                    )
+                    if h == 1 and i >= E_LAG:
+                        transpose_e(i - E_LAG, j)
+                    if h == 0 and V_STEP <= i < V_STEP + 4:
+                        transpose_v(i - V_STEP, j)
+                    if h == 0 and i == RB_STEP:
+                        spread_inverse(0, j)
+                    if h == 0 and i == BN_STEP and j == 0:
+                        bn_t = aux_ps.tile([P, P], BF16, name="bn_t", tag="aux")
+                        nc.tensor.transpose(bn_t[:], bn_rows[:], ident_bf16[:])
+
+            nc.vector.tensor_reduce(
+                out=half_max[:, i, 0:1], in_=s_bank[(i, 0)][:], axis=AXIS.X, op=ALU.max
+            )
+            if i == BN_STEP:
+                nc.vector.tensor_copy(out=bn_cols[:], in_=bn_t[:, 0 : 4 * C_CHUNKS])
+                gamma_c = bn_cols[:, 0:C_CHUNKS]
+                beta_c = bn_cols[:, C_CHUNKS : 2 * C_CHUNKS]
+                mean_c = bn_cols[:, 2 * C_CHUNKS : 3 * C_CHUNKS]
+                var_c = bn_cols[:, 3 * C_CHUNKS : 4 * C_CHUNKS]
+                nc.gpsimd.tensor_scalar_add(out=bn_var_eps[:], in0=var_c, scalar1=EPS)
+                nc.gpsimd.tensor_tensor(
+                    out=bn_rstd[:], in0=bn_var_eps[:], in1=minus_half[:], op=ALU.pow
+                )
+                nc.gpsimd.tensor_tensor(out=bn_scale[:], in0=gamma_c, in1=bn_rstd[:], op=ALU.mult)
+                nc.gpsimd.tensor_tensor(out=bn_shift[:], in0=mean_c, in1=bn_scale[:], op=ALU.mult)
+                nc.gpsimd.tensor_tensor(
+                    out=bn_bias[:], in0=beta_c, in1=bn_shift[:], op=ALU.subtract
+                )
+            if V_STEP <= i < V_STEP + 4:
+                evacuate_v(i - V_STEP)
+            if V_STEP + 4 <= i < V_STEP + 4 + K_PASSES:
+                quantise_v(i - V_STEP - 4)
+            nc.vector.tensor_reduce(
+                out=half_max[:, i, 1:2], in_=s_bank[(i, 1)][:], axis=AXIS.X, op=ALU.max
+            )
+            nc.vector.tensor_reduce(
+                out=neg_max[:, i : i + 1], in_=half_max[:, i, :], axis=AXIS.X, op=ALU.max,
+                negate=True,
+            )
+
+            if i >= E_LAG:
+                evacuate_e(i - E_LAG)
+            if i == RB_STEP:
+                evacuate_inverse(0)
+            e_sb[i] = ring.tile([P, PIXELS], BF16, name="e_sb", tag="e_sb")
+            for h in range(2):
+                nc.scalar.activation(
+                    out=e_sb[i][:, h * HALF : (h + 1) * HALF],
+                    in_=s_bank[(i, h)][:],
+                    func=ACT.Exp,
+                    bias=neg_max[:, i : i + 1],
+                    scale=1.0,
+                    accum_out=half_sum[:, i, h : h + 1],
+                )
+
+            if i >= E_LAG:
+                quantise_e(i - E_LAG)
+            if i == RB_STEP - 1:
+                invert_row_sums(0)
+
+        for c in range(2 * K_PASSES):
+            transpose_e(N_TILES - 2, c)
+        evacuate_e(N_TILES - 2)
+        for i in range(N_TILES + W_LAG - 1):
+            if i == LAST_E_ROUND:
+                for c in range(2 * K_PASSES):
+                    transpose_e(N_TILES - 1, c)
+                for r in range(4):
+                    spread_inverse(1, r)
+                evacuate_e(N_TILES - 1)
+                evacuate_inverse(1)
+            if i < N_TILES:
+                attend(i)
+                normalise(i)
+            if i == LAST_E_ROUND - 2:
+                invert_row_sums(1)
+            if i == LAST_E_ROUND - 1:
+                quantise_e(N_TILES - 2)
+            if i == LAST_E_ROUND:
+                quantise_e(N_TILES - 1)
+            if 1 <= i <= N_TILES:
+                quantise_ctx(i - 1)
+            group, odd = divmod(i - W_LAG, GROUP)
+            if odd == 0 and 0 <= group < N_GROUPS:
+                project(group)

@@ -27,8 +27,8 @@ GROUP_COLS = GROUP * P
 N_GROUPS = N_TILES // GROUP
 E_LAG = 2
 BN_STEP = 1
-V_STEP = 2
-RB_STEP = 6
+V_STEP = 3
+RB_STEP = 7
 LAST_E_ROUND = 3
 W_LAG = 4
 
@@ -49,8 +49,7 @@ def tile_objectattention_pa_kernel(
         ring = ctx.enter_context(tc.tile_pool(name="ring", bufs=3))
         y_pool = ctx.enter_context(tc.tile_pool(name="y_pool", bufs=N_GROUPS))
         acc_ps = ctx.enter_context(tc.psum_pool(name="acc_ps", bufs=4))
-        et_ps = ctx.enter_context(tc.psum_pool(name="et_ps", bufs=2))
-        aux_ps = ctx.enter_context(tc.psum_pool(name="aux_ps", bufs=2))
+        aux_ps = ctx.enter_context(tc.psum_pool(name="aux_ps", bufs=4))
         ctx.enter_context(tc.manual_schedule())
 
         q_sb = keep.tile([P, C_CHUNKS, PIXELS], BF16)
@@ -128,9 +127,9 @@ def tile_objectattention_pa_kernel(
         ctx_grouped = {}
         v_words = v_sb[:].bitcast(F32)
 
-        def transpose_e(i, c):
+        def transpose_e(i, c, banks):
             if c == 0:
-                e_t[i] = et_ps.tile([P, 2 * K_PASSES, P], F32, name="e_t", tag="e_t")
+                e_t[i] = banks.tile([P, 2 * K_PASSES, P], F32, name="e_t", tag="bank")
             nc.tensor.transpose(
                 e_t[i][:, c, :], e_sb[i][:].bitcast(F32)[:, c * P : (c + 1) * P], ident_f32[:]
             )
@@ -156,7 +155,7 @@ def tile_objectattention_pa_kernel(
             u, second = divmod(r, 2)
             t = 2 * pair + second
             if r == 0:
-                v_t[bank] = aux_ps.tile([P, 2, 2 * P], F32, name="v_t", tag="aux")
+                v_t[bank] = aux_ps.tile([P, 2, 2 * P], F32, name="v_t", tag="bank")
             first_word = (2 * g + u) * P
             nc.tensor.transpose(
                 v_t[bank][:, u, second * P : (second + 1) * P],
@@ -188,7 +187,7 @@ def tile_objectattention_pa_kernel(
 
         def spread_inverse(half, r):
             if r == 0:
-                inv_t[half] = aux_ps.tile([P, 4, P], F32, name="inv_t", tag="aux")
+                inv_t[half] = aux_ps.tile([P, 4, P], F32, name="inv_t", tag="bank")
             i = half * 4 + r
             nc.tensor.transpose(
                 inv_t[half][:, r, :], row_inv[:, i : i + 1].to_broadcast([P, P]), ident_f32[:]
@@ -201,7 +200,7 @@ def tile_objectattention_pa_kernel(
             )
 
         def attend(i):
-            ctx_ps[i] = aux_ps.tile([P, PACK, P], F32, name="ctx_ps", tag="aux")
+            ctx_ps[i] = aux_ps.tile([P, PACK, P], F32, name="ctx_ps", tag="bank")
             for t in range(PACK):
                 for g in range(K_PASSES):
                     nc.tensor.matmul_mx(
@@ -236,7 +235,7 @@ def tile_objectattention_pa_kernel(
             queries = slice(group * GROUP_COLS, (group + 1) * GROUP_COLS)
             y_sb = y_pool.tile([P, C_CHUNKS, GROUP_COLS], F32, name="y_sb", tag="y_sb")
             for pair in range(C_CHUNKS // 2):
-                y_bank = acc_ps.tile([P, 2, GROUP_COLS], F32, name="y_bank", tag="acc")
+                y_bank = acc_ps.tile([P, 2, GROUP_COLS], F32, name="y_bank", tag="bank")
                 for second in range(2):
                     j = 2 * pair + second
                     nc.tensor.matmul_mx(
@@ -257,11 +256,11 @@ def tile_objectattention_pa_kernel(
                         bias=bn_bias[:, j : j + 1],
                         scale=bn_scale[:, j : j + 1],
                     )
-            nc.sync.dma_start(out=out_view[:, :, queries], in_=y_sb[:])
+                    nc.sync.dma_start(out=out_view[:, j, queries], in_=y_sb[:, j, :])
 
         for i in range(N_TILES):
             for h in range(2):
-                s_bank[(i, h)] = acc_ps.tile([P, HALF], F32, name="s_bank", tag="acc")
+                s_bank[(i, h)] = acc_ps.tile([P, HALF], F32, name="s_bank", tag="bank")
                 for j in range(C_CHUNKS):
                     nc.tensor.matmul(
                         out=s_bank[(i, h)][:],
@@ -271,13 +270,13 @@ def tile_objectattention_pa_kernel(
                         stop=(j == C_CHUNKS - 1),
                     )
                     if h == 1 and i >= E_LAG:
-                        transpose_e(i - E_LAG, j)
+                        transpose_e(i - E_LAG, j, aux_ps)
                     if h == 0 and V_STEP <= i < V_STEP + 4:
                         transpose_v(i - V_STEP, j)
                     if h == 0 and i == RB_STEP:
                         spread_inverse(0, j)
                     if h == 0 and i == BN_STEP and j == 0:
-                        bn_t = aux_ps.tile([P, P], BF16, name="bn_t", tag="aux")
+                        bn_t = aux_ps.tile([P, P], BF16, name="bn_t", tag="bank")
                         nc.tensor.transpose(bn_t[:], bn_rows[:], ident_bf16[:])
 
             nc.vector.tensor_reduce(
@@ -300,8 +299,8 @@ def tile_objectattention_pa_kernel(
                 )
             if V_STEP <= i < V_STEP + 4:
                 evacuate_v(i - V_STEP)
-            if V_STEP + 4 <= i < V_STEP + 4 + K_PASSES:
-                quantise_v(i - V_STEP - 4)
+            if i == V_STEP + 2 or i == V_STEP + 4:
+                quantise_v((i - V_STEP - 2) // 2)
             nc.vector.tensor_reduce(
                 out=half_max[:, i, 1:2], in_=s_bank[(i, 1)][:], axis=AXIS.X, op=ALU.max
             )
@@ -310,10 +309,10 @@ def tile_objectattention_pa_kernel(
                 negate=True,
             )
 
-            if i >= E_LAG:
-                evacuate_e(i - E_LAG)
             if i == RB_STEP:
                 evacuate_inverse(0)
+            if i >= E_LAG:
+                evacuate_e(i - E_LAG)
             e_sb[i] = ring.tile([P, PIXELS], BF16, name="e_sb", tag="e_sb")
             for h in range(2):
                 nc.scalar.activation(
@@ -327,16 +326,16 @@ def tile_objectattention_pa_kernel(
 
             if i >= E_LAG:
                 quantise_e(i - E_LAG)
-            if i == RB_STEP - 1:
+            if i == RB_STEP - 2:
                 invert_row_sums(0)
 
         for c in range(2 * K_PASSES):
-            transpose_e(N_TILES - 2, c)
+            transpose_e(N_TILES - 2, c, acc_ps)
         evacuate_e(N_TILES - 2)
         for i in range(N_TILES + W_LAG - 1):
             if i == LAST_E_ROUND:
                 for c in range(2 * K_PASSES):
-                    transpose_e(N_TILES - 1, c)
+                    transpose_e(N_TILES - 1, c, acc_ps)
                 for r in range(4):
                     spread_inverse(1, r)
                 evacuate_e(N_TILES - 1)

@@ -26,7 +26,9 @@ GROUP = 2
 GROUP_COLS = GROUP * P
 N_GROUPS = N_TILES // GROUP
 E_LAG = 2
-BN_STEP = 1
+WARM_MATMULS = 6
+FIRST_TILES = 2
+BN_STEP = 4
 V_STEP = 3
 RB_STEP = 7
 LAST_E_ROUND = 3
@@ -48,8 +50,8 @@ def tile_objectattention_pa_kernel(
         keep = ctx.enter_context(tc.tile_pool(name="keep", bufs=1))
         ring = ctx.enter_context(tc.tile_pool(name="ring", bufs=3))
         y_pool = ctx.enter_context(tc.tile_pool(name="y_pool", bufs=N_GROUPS))
-        acc_ps = ctx.enter_context(tc.psum_pool(name="acc_ps", bufs=4))
-        aux_ps = ctx.enter_context(tc.psum_pool(name="aux_ps", bufs=4))
+        acc_ps = ctx.enter_context(tc.psum_pool(name="acc_ps", bufs=5))
+        aux_ps = ctx.enter_context(tc.psum_pool(name="aux_ps", bufs=3))
         ctx.enter_context(tc.manual_schedule())
 
         q_sb = keep.tile([P, C_CHUNKS, PIXELS], BF16)
@@ -65,6 +67,7 @@ def tile_objectattention_pa_kernel(
         bn_scale = keep.tile([P, C_CHUNKS], F32)
         bn_shift = keep.tile([P, C_CHUNKS], F32)
         bn_bias = keep.tile([P, C_CHUNKS], F32)
+        zeros = keep.tile([P, HALF], BF16)
         table_in = keep.tile([P, 1], F32)
         table_out = keep.tile([P, 1], F32)
         half_max = keep.tile([P, N_TILES, 2], F32)
@@ -83,24 +86,36 @@ def tile_objectattention_pa_kernel(
         c_codes = keep.tile([P, PIXELS], U32, align_bytes=64)
         c_plane = keep.tile([P, PIXELS], U8, align_bytes=64)
 
+        nc.vector.memset(zeros[:], 0.0)
+        warm_bank = acc_ps.tile([P, HALF], F32, name="warm_bank", tag="bank")
+        for repeat in range(WARM_MATMULS):
+            nc.tensor.matmul(
+                out=warm_bank[:], lhsT=zeros[:, 0:P], rhs=zeros[:], start=True, stop=True
+            )
+
         nc.vector.memset(table_in[:], 0.0)
         nc.vector.memset(bn_rows[:], 0.0)
         nc.vector.memset(w_plane[:].bitcast(I32), 0)
         nc.scalar.activation(out=table_out[:], in_=table_in[:], func=ACT.Exp)
-        make_identity(nc, ident_bf16[:])
         make_identity(nc, ident_f32[:])
-        nc.gpsimd.memset(minus_half[:], -0.5)
-
-        first_q = GROUP_COLS
-        for j in range(C_CHUNKS):
-            nc.sync.dma_start(out=q_sb[:, j, 0:first_q], in_=q_view[:, j, 0:first_q])
-            nc.sync.dma_start(out=k_sb[:, j, 0:HALF], in_=k_view[:, j, 0:HALF])
-        for j in range(C_CHUNKS):
-            nc.sync.dma_start(out=k_sb[:, j, HALF:PIXELS], in_=k_view[:, j, HALF:PIXELS])
+        make_identity(nc, ident_bf16[:])
         for row, vector in enumerate((gamma, beta, mean, var)):
-            nc.sync.dma_start(
+            nc.gpsimd.dma_start(
                 out=bn_rows[C_CHUNKS * row : C_CHUNKS * (row + 1), :],
                 in_=vector.rearrange("(j p) -> j p", p=P),
+            )
+        nc.gpsimd.memset(minus_half[:], -0.5)
+
+        first_q = FIRST_TILES * P
+        for j in range(0, C_CHUNKS, 2):
+            nc.sync.dma_start(
+                out=q_sb[:, j : j + 2, 0:first_q], in_=q_view[:, j : j + 2, 0:first_q]
+            )
+            nc.sync.dma_start(out=k_sb[:, j, 0:HALF], in_=k_view[:, j, 0:HALF])
+            nc.sync.dma_start(out=k_sb[:, j + 1, 0:HALF], in_=k_view[:, j + 1, 0:HALF])
+        for j in range(0, C_CHUNKS, 2):
+            nc.sync.dma_start(
+                out=k_sb[:, j : j + 2, HALF:PIXELS], in_=k_view[:, j : j + 2, HALF:PIXELS]
             )
         nc.sync.dma_start(out=q_sb[:, :, first_q:HALF], in_=q_view[:, :, first_q:HALF])
         for g in range(K_PASSES):
@@ -258,61 +273,29 @@ def tile_objectattention_pa_kernel(
                     )
                     nc.sync.dma_start(out=out_view[:, j, queries], in_=y_sb[:, j, :])
 
-        for i in range(N_TILES):
-            for h in range(2):
+        def score_matmul(i, h, j):
+            if j == 0:
                 s_bank[(i, h)] = acc_ps.tile([P, HALF], F32, name="s_bank", tag="bank")
-                for j in range(C_CHUNKS):
-                    nc.tensor.matmul(
-                        out=s_bank[(i, h)][:],
-                        lhsT=q_sb[:, j, i * P : (i + 1) * P],
-                        rhs=k_sb[:, j, h * HALF : (h + 1) * HALF],
-                        start=(j == 0),
-                        stop=(j == C_CHUNKS - 1),
-                    )
-                    if h == 1 and i >= E_LAG:
-                        transpose_e(i - E_LAG, j, aux_ps)
-                    if h == 0 and V_STEP <= i < V_STEP + 4:
-                        transpose_v(i - V_STEP, j)
-                    if h == 0 and i == RB_STEP:
-                        spread_inverse(0, j)
-                    if h == 0 and i == BN_STEP and j == 0:
-                        bn_t = aux_ps.tile([P, P], BF16, name="bn_t", tag="bank")
-                        nc.tensor.transpose(bn_t[:], bn_rows[:], ident_bf16[:])
+            nc.tensor.matmul(
+                out=s_bank[(i, h)][:],
+                lhsT=q_sb[:, j, i * P : (i + 1) * P],
+                rhs=k_sb[:, j, h * HALF : (h + 1) * HALF],
+                start=(j == 0),
+                stop=(j == C_CHUNKS - 1),
+            )
 
+        def half_maximum(i, h):
             nc.vector.tensor_reduce(
-                out=half_max[:, i, 0:1], in_=s_bank[(i, 0)][:], axis=AXIS.X, op=ALU.max
+                out=half_max[:, i, h : h + 1], in_=s_bank[(i, h)][:], axis=AXIS.X, op=ALU.max
             )
-            if i == BN_STEP:
-                nc.vector.tensor_copy(out=bn_cols[:], in_=bn_t[:, 0 : 4 * C_CHUNKS])
-                gamma_c = bn_cols[:, 0:C_CHUNKS]
-                beta_c = bn_cols[:, C_CHUNKS : 2 * C_CHUNKS]
-                mean_c = bn_cols[:, 2 * C_CHUNKS : 3 * C_CHUNKS]
-                var_c = bn_cols[:, 3 * C_CHUNKS : 4 * C_CHUNKS]
-                nc.gpsimd.tensor_scalar_add(out=bn_var_eps[:], in0=var_c, scalar1=EPS)
-                nc.gpsimd.tensor_tensor(
-                    out=bn_rstd[:], in0=bn_var_eps[:], in1=minus_half[:], op=ALU.pow
-                )
-                nc.gpsimd.tensor_tensor(out=bn_scale[:], in0=gamma_c, in1=bn_rstd[:], op=ALU.mult)
-                nc.gpsimd.tensor_tensor(out=bn_shift[:], in0=mean_c, in1=bn_scale[:], op=ALU.mult)
-                nc.gpsimd.tensor_tensor(
-                    out=bn_bias[:], in0=beta_c, in1=bn_shift[:], op=ALU.subtract
-                )
-            if V_STEP <= i < V_STEP + 4:
-                evacuate_v(i - V_STEP)
-            if i == V_STEP + 2 or i == V_STEP + 4:
-                quantise_v((i - V_STEP - 2) // 2)
-            nc.vector.tensor_reduce(
-                out=half_max[:, i, 1:2], in_=s_bank[(i, 1)][:], axis=AXIS.X, op=ALU.max
-            )
+
+        def negated_maximum(i):
             nc.vector.tensor_reduce(
                 out=neg_max[:, i : i + 1], in_=half_max[:, i, :], axis=AXIS.X, op=ALU.max,
                 negate=True,
             )
 
-            if i == RB_STEP:
-                evacuate_inverse(0)
-            if i >= E_LAG:
-                evacuate_e(i - E_LAG)
+        def exponentials(i):
             e_sb[i] = ring.tile([P, PIXELS], BF16, name="e_sb", tag="e_sb")
             for h in range(2):
                 nc.scalar.activation(
@@ -324,6 +307,53 @@ def tile_objectattention_pa_kernel(
                     accum_out=half_sum[:, i, h : h + 1],
                 )
 
+        def batch_norm_constants():
+            nc.vector.tensor_copy(out=bn_cols[:], in_=bn_t[:, 0 : 4 * C_CHUNKS])
+            gamma_c = bn_cols[:, 0:C_CHUNKS]
+            beta_c = bn_cols[:, C_CHUNKS : 2 * C_CHUNKS]
+            mean_c = bn_cols[:, 2 * C_CHUNKS : 3 * C_CHUNKS]
+            var_c = bn_cols[:, 3 * C_CHUNKS : 4 * C_CHUNKS]
+            nc.gpsimd.tensor_scalar_add(out=bn_var_eps[:], in0=var_c, scalar1=EPS)
+            nc.gpsimd.tensor_tensor(out=bn_rstd[:], in0=bn_var_eps[:], in1=minus_half[:], op=ALU.pow)
+            nc.gpsimd.tensor_tensor(out=bn_scale[:], in0=gamma_c, in1=bn_rstd[:], op=ALU.mult)
+            nc.gpsimd.tensor_tensor(out=bn_shift[:], in0=mean_c, in1=bn_scale[:], op=ALU.mult)
+            nc.gpsimd.tensor_tensor(out=bn_bias[:], in0=beta_c, in1=bn_shift[:], op=ALU.subtract)
+
+        for j in range(C_CHUNKS):
+            for i in range(FIRST_TILES):
+                score_matmul(i, 0, j)
+
+        for i in range(N_TILES):
+            for h in range(2):
+                for j in range(C_CHUNKS):
+                    if h == 1 or i >= FIRST_TILES:
+                        score_matmul(i, h, j)
+                    if h == 1 and i >= E_LAG:
+                        transpose_e(i - E_LAG, j, aux_ps)
+                    if h == 0 and V_STEP <= i < V_STEP + 4:
+                        transpose_v(i - V_STEP, j)
+                    if h == 0 and i == RB_STEP:
+                        spread_inverse(0, j)
+            if i == BN_STEP:
+                bn_t = aux_ps.tile([P, P], BF16, name="bn_t", tag="bank")
+                nc.tensor.transpose(bn_t[:], bn_rows[:], ident_bf16[:])
+
+            half_maximum(i, 0)
+            if V_STEP <= i < V_STEP + 4:
+                evacuate_v(i - V_STEP)
+            if i == V_STEP + 2 or i == V_STEP + 4:
+                quantise_v((i - V_STEP - 2) // 2)
+            half_maximum(i, 1)
+            negated_maximum(i)
+
+            if i == RB_STEP:
+                evacuate_inverse(0)
+            if i >= E_LAG:
+                evacuate_e(i - E_LAG)
+            exponentials(i)
+
+            if i == BN_STEP:
+                batch_norm_constants()
             if i >= E_LAG:
                 quantise_e(i - E_LAG)
             if i == RB_STEP - 2:
@@ -332,7 +362,7 @@ def tile_objectattention_pa_kernel(
         for c in range(2 * K_PASSES):
             transpose_e(N_TILES - 2, c, acc_ps)
         evacuate_e(N_TILES - 2)
-        for i in range(N_TILES + W_LAG - 1):
+        for i in range(N_TILES + W_LAG):
             if i == LAST_E_ROUND:
                 for c in range(2 * K_PASSES):
                     transpose_e(N_TILES - 1, c, acc_ps)

@@ -26,9 +26,7 @@ GROUP = 2
 GROUP_COLS = GROUP * P
 N_GROUPS = N_TILES // GROUP
 E_LAG = 2
-WARM_MATMULS = 6
-FIRST_TILES = 2
-BN_STEP = 4
+BN_STEP = 1
 V_STEP = 3
 RB_STEP = 7
 LAST_E_ROUND = 3
@@ -50,8 +48,8 @@ def tile_objectattention_pa_kernel(
         keep = ctx.enter_context(tc.tile_pool(name="keep", bufs=1))
         ring = ctx.enter_context(tc.tile_pool(name="ring", bufs=3))
         y_pool = ctx.enter_context(tc.tile_pool(name="y_pool", bufs=N_GROUPS))
-        acc_ps = ctx.enter_context(tc.psum_pool(name="acc_ps", bufs=5))
-        aux_ps = ctx.enter_context(tc.psum_pool(name="aux_ps", bufs=3))
+        acc_ps = ctx.enter_context(tc.psum_pool(name="acc_ps", bufs=4))
+        aux_ps = ctx.enter_context(tc.psum_pool(name="aux_ps", bufs=4))
         ctx.enter_context(tc.manual_schedule())
 
         q_sb = keep.tile([P, C_CHUNKS, PIXELS], BF16)
@@ -67,10 +65,9 @@ def tile_objectattention_pa_kernel(
         bn_scale = keep.tile([P, C_CHUNKS], F32)
         bn_shift = keep.tile([P, C_CHUNKS], F32)
         bn_bias = keep.tile([P, C_CHUNKS], F32)
-        zeros = keep.tile([P, HALF], BF16)
         table_in = keep.tile([P, 1], F32)
         table_out = keep.tile([P, 1], F32)
-        half_max = keep.tile([P, N_TILES, 2], F32)
+        half_max = keep.tile([P, N_TILES], F32)
         neg_max = keep.tile([P, N_TILES], F32)
         half_sum = keep.tile([P, N_TILES, 2], F32)
         row_sum = keep.tile([P, N_TILES], F32)
@@ -86,36 +83,24 @@ def tile_objectattention_pa_kernel(
         c_codes = keep.tile([P, PIXELS], U32, align_bytes=64)
         c_plane = keep.tile([P, PIXELS], U8, align_bytes=64)
 
-        nc.vector.memset(zeros[:], 0.0)
-        warm_bank = acc_ps.tile([P, HALF], F32, name="warm_bank", tag="bank")
-        for repeat in range(WARM_MATMULS):
-            nc.tensor.matmul(
-                out=warm_bank[:], lhsT=zeros[:, 0:P], rhs=zeros[:], start=True, stop=True
-            )
-
         nc.vector.memset(table_in[:], 0.0)
         nc.vector.memset(bn_rows[:], 0.0)
         nc.vector.memset(w_plane[:].bitcast(I32), 0)
         nc.scalar.activation(out=table_out[:], in_=table_in[:], func=ACT.Exp)
-        make_identity(nc, ident_f32[:])
         make_identity(nc, ident_bf16[:])
-        for row, vector in enumerate((gamma, beta, mean, var)):
-            nc.gpsimd.dma_start(
-                out=bn_rows[C_CHUNKS * row : C_CHUNKS * (row + 1), :],
-                in_=vector.rearrange("(j p) -> j p", p=P),
-            )
+        make_identity(nc, ident_f32[:])
         nc.gpsimd.memset(minus_half[:], -0.5)
 
-        first_q = FIRST_TILES * P
-        for j in range(0, C_CHUNKS, 2):
-            nc.sync.dma_start(
-                out=q_sb[:, j : j + 2, 0:first_q], in_=q_view[:, j : j + 2, 0:first_q]
-            )
+        first_q = GROUP_COLS
+        for j in range(C_CHUNKS):
+            nc.sync.dma_start(out=q_sb[:, j, 0:first_q], in_=q_view[:, j, 0:first_q])
             nc.sync.dma_start(out=k_sb[:, j, 0:HALF], in_=k_view[:, j, 0:HALF])
-            nc.sync.dma_start(out=k_sb[:, j + 1, 0:HALF], in_=k_view[:, j + 1, 0:HALF])
-        for j in range(0, C_CHUNKS, 2):
+        for j in range(C_CHUNKS):
+            nc.sync.dma_start(out=k_sb[:, j, HALF:PIXELS], in_=k_view[:, j, HALF:PIXELS])
+        for row, vector in enumerate((gamma, beta, mean, var)):
             nc.sync.dma_start(
-                out=k_sb[:, j : j + 2, HALF:PIXELS], in_=k_view[:, j : j + 2, HALF:PIXELS]
+                out=bn_rows[C_CHUNKS * row : C_CHUNKS * (row + 1), :],
+                in_=vector.rearrange("(j p) -> j p", p=P),
             )
         nc.sync.dma_start(out=q_sb[:, :, first_q:HALF], in_=q_view[:, :, first_q:HALF])
         for g in range(K_PASSES):
@@ -273,29 +258,65 @@ def tile_objectattention_pa_kernel(
                     )
                     nc.sync.dma_start(out=out_view[:, j, queries], in_=y_sb[:, j, :])
 
-        def score_matmul(i, h, j):
-            if j == 0:
+        for i in range(N_TILES):
+            for h in range(2):
                 s_bank[(i, h)] = acc_ps.tile([P, HALF], F32, name="s_bank", tag="bank")
-            nc.tensor.matmul(
-                out=s_bank[(i, h)][:],
-                lhsT=q_sb[:, j, i * P : (i + 1) * P],
-                rhs=k_sb[:, j, h * HALF : (h + 1) * HALF],
-                start=(j == 0),
-                stop=(j == C_CHUNKS - 1),
-            )
+                for j in range(C_CHUNKS):
+                    nc.tensor.matmul(
+                        out=s_bank[(i, h)][:],
+                        lhsT=q_sb[:, j, i * P : (i + 1) * P],
+                        rhs=k_sb[:, j, h * HALF : (h + 1) * HALF],
+                        start=(j == 0),
+                        stop=(j == C_CHUNKS - 1),
+                    )
+                    if h == 1 and i >= E_LAG:
+                        transpose_e(i - E_LAG, j, aux_ps)
+                    if h == 0 and V_STEP <= i < V_STEP + 4:
+                        transpose_v(i - V_STEP, j)
+                    if h == 0 and i == RB_STEP:
+                        spread_inverse(0, j)
+                    if h == 0 and i == BN_STEP and j == 0:
+                        bn_t = aux_ps.tile([P, P], BF16, name="bn_t", tag="bank")
+                        nc.tensor.transpose(bn_t[:], bn_rows[:], ident_bf16[:])
 
-        def half_maximum(i, h):
             nc.vector.tensor_reduce(
-                out=half_max[:, i, h : h + 1], in_=s_bank[(i, h)][:], axis=AXIS.X, op=ALU.max
-            )
-
-        def negated_maximum(i):
-            nc.vector.tensor_reduce(
-                out=neg_max[:, i : i + 1], in_=half_max[:, i, :], axis=AXIS.X, op=ALU.max,
+                out=half_max[:, i : i + 1], in_=s_bank[(i, 0)][:], axis=AXIS.X, op=ALU.max,
                 negate=True,
             )
+            if i == BN_STEP:
+                nc.vector.tensor_copy(out=bn_cols[:], in_=bn_t[:, 0 : 4 * C_CHUNKS])
+                gamma_c = bn_cols[:, 0:C_CHUNKS]
+                beta_c = bn_cols[:, C_CHUNKS : 2 * C_CHUNKS]
+                mean_c = bn_cols[:, 2 * C_CHUNKS : 3 * C_CHUNKS]
+                var_c = bn_cols[:, 3 * C_CHUNKS : 4 * C_CHUNKS]
+                nc.gpsimd.tensor_scalar_add(out=bn_var_eps[:], in0=var_c, scalar1=EPS)
+                nc.gpsimd.tensor_tensor(
+                    out=bn_rstd[:], in0=bn_var_eps[:], in1=minus_half[:], op=ALU.pow
+                )
+                nc.gpsimd.tensor_tensor(out=bn_scale[:], in0=gamma_c, in1=bn_rstd[:], op=ALU.mult)
+                nc.gpsimd.tensor_tensor(out=bn_shift[:], in0=mean_c, in1=bn_scale[:], op=ALU.mult)
+                nc.gpsimd.tensor_tensor(
+                    out=bn_bias[:], in0=beta_c, in1=bn_shift[:], op=ALU.subtract
+                )
+            if V_STEP <= i < V_STEP + 4:
+                evacuate_v(i - V_STEP)
+            if i == V_STEP + 2 or i == V_STEP + 4:
+                quantise_v((i - V_STEP - 2) // 2)
+            negated = ring.tile([P, HALF], BF16, name="negated", tag="negated")
+            nc.vector.tensor_scalar(
+                out=negated[:],
+                in0=s_bank[(i, 1)][:],
+                scalar1=-1.0,
+                scalar2=half_max[:, i : i + 1],
+                op0=ALU.mult,
+                op1=ALU.min,
+                accum_out=neg_max[:, i : i + 1],
+            )
 
-        def exponentials(i):
+            if i == RB_STEP:
+                evacuate_inverse(0)
+            if i >= E_LAG:
+                evacuate_e(i - E_LAG)
             e_sb[i] = ring.tile([P, PIXELS], BF16, name="e_sb", tag="e_sb")
             for h in range(2):
                 nc.scalar.activation(
@@ -307,53 +328,6 @@ def tile_objectattention_pa_kernel(
                     accum_out=half_sum[:, i, h : h + 1],
                 )
 
-        def batch_norm_constants():
-            nc.vector.tensor_copy(out=bn_cols[:], in_=bn_t[:, 0 : 4 * C_CHUNKS])
-            gamma_c = bn_cols[:, 0:C_CHUNKS]
-            beta_c = bn_cols[:, C_CHUNKS : 2 * C_CHUNKS]
-            mean_c = bn_cols[:, 2 * C_CHUNKS : 3 * C_CHUNKS]
-            var_c = bn_cols[:, 3 * C_CHUNKS : 4 * C_CHUNKS]
-            nc.gpsimd.tensor_scalar_add(out=bn_var_eps[:], in0=var_c, scalar1=EPS)
-            nc.gpsimd.tensor_tensor(out=bn_rstd[:], in0=bn_var_eps[:], in1=minus_half[:], op=ALU.pow)
-            nc.gpsimd.tensor_tensor(out=bn_scale[:], in0=gamma_c, in1=bn_rstd[:], op=ALU.mult)
-            nc.gpsimd.tensor_tensor(out=bn_shift[:], in0=mean_c, in1=bn_scale[:], op=ALU.mult)
-            nc.gpsimd.tensor_tensor(out=bn_bias[:], in0=beta_c, in1=bn_shift[:], op=ALU.subtract)
-
-        for j in range(C_CHUNKS):
-            for i in range(FIRST_TILES):
-                score_matmul(i, 0, j)
-
-        for i in range(N_TILES):
-            for h in range(2):
-                for j in range(C_CHUNKS):
-                    if h == 1 or i >= FIRST_TILES:
-                        score_matmul(i, h, j)
-                    if h == 1 and i >= E_LAG:
-                        transpose_e(i - E_LAG, j, aux_ps)
-                    if h == 0 and V_STEP <= i < V_STEP + 4:
-                        transpose_v(i - V_STEP, j)
-                    if h == 0 and i == RB_STEP:
-                        spread_inverse(0, j)
-            if i == BN_STEP:
-                bn_t = aux_ps.tile([P, P], BF16, name="bn_t", tag="bank")
-                nc.tensor.transpose(bn_t[:], bn_rows[:], ident_bf16[:])
-
-            half_maximum(i, 0)
-            if V_STEP <= i < V_STEP + 4:
-                evacuate_v(i - V_STEP)
-            if i == V_STEP + 2 or i == V_STEP + 4:
-                quantise_v((i - V_STEP - 2) // 2)
-            half_maximum(i, 1)
-            negated_maximum(i)
-
-            if i == RB_STEP:
-                evacuate_inverse(0)
-            if i >= E_LAG:
-                evacuate_e(i - E_LAG)
-            exponentials(i)
-
-            if i == BN_STEP:
-                batch_norm_constants()
             if i >= E_LAG:
                 quantise_e(i - E_LAG)
             if i == RB_STEP - 2:
@@ -362,7 +336,7 @@ def tile_objectattention_pa_kernel(
         for c in range(2 * K_PASSES):
             transpose_e(N_TILES - 2, c, acc_ps)
         evacuate_e(N_TILES - 2)
-        for i in range(N_TILES + W_LAG):
+        for i in range(N_TILES + W_LAG - 1):
             if i == LAST_E_ROUND:
                 for c in range(2 * K_PASSES):
                     transpose_e(N_TILES - 1, c, acc_ps)

@@ -30,6 +30,7 @@ BN_STEP = 1
 V_STEP = 3
 RB_STEP = 7
 LAST_E_ROUND = 3
+WARM_PASSES = 3
 W_LAG = 4
 
 FLOPS = 2 * PIXELS * PIXELS * CHANNELS * 2 + 2 * CHANNELS * CHANNELS * PIXELS
@@ -65,6 +66,7 @@ def tile_objectattention_pa_kernel(
         bn_scale = keep.tile([P, C_CHUNKS], F32)
         bn_shift = keep.tile([P, C_CHUNKS], F32)
         bn_bias = keep.tile([P, C_CHUNKS], F32)
+        warm_in = keep.tile([P, HALF], BF16)
         table_in = keep.tile([P, 1], F32)
         table_out = keep.tile([P, 1], F32)
         half_max = keep.tile([P, N_TILES], F32)
@@ -83,6 +85,7 @@ def tile_objectattention_pa_kernel(
         c_codes = keep.tile([P, PIXELS], U32, align_bytes=64)
         c_plane = keep.tile([P, PIXELS], U8, align_bytes=64)
 
+        nc.vector.memset(warm_in[:].bitcast(I32), 0)
         nc.vector.memset(table_in[:], 0.0)
         nc.vector.memset(bn_rows[:], 0.0)
         nc.vector.memset(w_plane[:].bitcast(I32), 0)
@@ -90,6 +93,12 @@ def tile_objectattention_pa_kernel(
         make_identity(nc, ident_bf16[:])
         make_identity(nc, ident_f32[:])
         nc.gpsimd.memset(minus_half[:], -0.5)
+
+        warm_ps = aux_ps.tile([P, HALF], F32, name="warm_ps", tag="bank")
+        for warm in range(WARM_PASSES):
+            nc.tensor.matmul(
+                out=warm_ps[:], lhsT=warm_in[:, 0:P], rhs=warm_in[:], start=True, stop=True
+            )
 
         first_q = GROUP_COLS
         for j in range(C_CHUNKS):

@@ -25,13 +25,8 @@ K_PASSES = PIXELS // (P * PACK)
 GROUP = 2
 GROUP_COLS = GROUP * P
 N_GROUPS = N_TILES // GROUP
-E_LAG = 2
-BN_STEP = 1
-V_STEP = 3
-RB_STEP = 7
-LAST_E_ROUND = 3
 WARM_PASSES = 3
-W_LAG = 4
+
 
 FLOPS = 2 * PIXELS * PIXELS * CHANNELS * 2 + 2 * CHANNELS * CHANNELS * PIXELS
 
@@ -48,7 +43,7 @@ def tile_objectattention_pa_kernel(
     with ExitStack() as ctx:
         keep = ctx.enter_context(tc.tile_pool(name="keep", bufs=1))
         ring = ctx.enter_context(tc.tile_pool(name="ring", bufs=3))
-        y_pool = ctx.enter_context(tc.tile_pool(name="y_pool", bufs=N_GROUPS))
+        y_pool = ctx.enter_context(tc.tile_pool(name="y_pool", bufs=8))
         acc_ps = ctx.enter_context(tc.psum_pool(name="acc_ps", bufs=4))
         aux_ps = ctx.enter_context(tc.psum_pool(name="aux_ps", bufs=4))
         ctx.enter_context(tc.manual_schedule())
@@ -104,17 +99,13 @@ def tile_objectattention_pa_kernel(
         for j in range(C_CHUNKS):
             nc.sync.dma_start(out=q_sb[:, j, 0:first_q], in_=q_view[:, j, 0:first_q])
             nc.sync.dma_start(out=k_sb[:, j, 0:HALF], in_=k_view[:, j, 0:HALF])
-        for j in range(C_CHUNKS):
-            nc.sync.dma_start(out=k_sb[:, j, HALF:PIXELS], in_=k_view[:, j, HALF:PIXELS])
-        for row, vector in enumerate((gamma, beta, mean, var)):
-            nc.sync.dma_start(
-                out=bn_rows[C_CHUNKS * row : C_CHUNKS * (row + 1), :],
-                in_=vector.rearrange("(j p) -> j p", p=P),
-            )
+        for pair in range(2):
+            chunks = slice(2 * pair, 2 * pair + 2)
+            nc.sync.dma_start(out=k_sb[:, chunks, HALF:PIXELS], in_=k_view[:, chunks, HALF:PIXELS])
         nc.sync.dma_start(out=q_sb[:, :, first_q:HALF], in_=q_view[:, :, first_q:HALF])
-        for g in range(K_PASSES):
-            keys = slice(g * HALF, (g + 1) * HALF)
-            nc.sync.dma_start(out=v_sb[:, :, keys], in_=v_view[:, :, keys])
+        for pair in range(2):
+            rows = slice(2 * pair, 2 * pair + 2)
+            nc.sync.dma_start(out=v_sb[:, rows, :], in_=v_view[:, rows, :])
         nc.sync.dma_start(out=q_sb[:, :, HALF:PIXELS], in_=q_view[:, :, HALF:PIXELS])
         nc.sync.dma_start(
             out=w_codes[:].bitcast(I32),
@@ -124,6 +115,11 @@ def tile_objectattention_pa_kernel(
             nc.sync.dma_start(
                 out=w_plane[32 * quad : 32 * quad + 4, :].bitcast(I32),
                 in_=w_up_scales[0, 4 * quad : 4 * quad + 4, :].bitcast(I32),
+            )
+        for row, vector in enumerate((gamma, beta, mean, var)):
+            nc.sync.dma_start(
+                out=bn_rows[C_CHUNKS * row : C_CHUNKS * (row + 1), :],
+                in_=vector.rearrange("(j p) -> j p", p=P),
             )
 
         s_bank = {}
@@ -143,11 +139,11 @@ def tile_objectattention_pa_kernel(
                 e_t[i][:, c, :], e_sb[i][:].bitcast(F32)[:, c * P : (c + 1) * P], ident_f32[:]
             )
 
-        def evacuate_e(i):
+        def evacuate_e(i, copy=nc.scalar.copy):
             e_grouped[i] = ring.tile(
                 [P, K_PASSES, P, PACK], BF16, name="e_grouped", tag="e_grouped", align_bytes=64
             )
-            nc.scalar.copy(
+            copy(
                 out=e_grouped[i][:].bitcast(F32),
                 in_=e_t[i][:].rearrange("p (g u) n -> p g n u", u=2),
             )
@@ -160,7 +156,7 @@ def tile_objectattention_pa_kernel(
             )
 
         def transpose_v(bank, r):
-            g, pair = divmod(bank, 2)
+            pair, g = divmod(bank, 2)
             u, second = divmod(r, 2)
             t = 2 * pair + second
             if r == 0:
@@ -172,10 +168,10 @@ def tile_objectattention_pa_kernel(
                 ident_f32[:],
             )
 
-        def evacuate_v(bank):
-            g, pair = divmod(bank, 2)
+        def evacuate_v(bank, copy):
+            pair, g = divmod(bank, 2)
             columns = slice(pair * 2 * P, (pair + 1) * 2 * P)
-            nc.vector.tensor_copy(
+            copy(
                 out=v_grouped[:, g, columns, :].bitcast(F32),
                 in_=v_t[bank][:].rearrange("p u c -> p c u"),
             )
@@ -187,16 +183,19 @@ def tile_objectattention_pa_kernel(
                 in_=v_grouped[:, g].rearrange("p c t -> p (c t)"),
             )
 
-        def invert_row_sums(half):
+        def sum_rows(half):
             tiles = slice(half * 4, (half + 1) * 4)
             nc.vector.tensor_reduce(
                 out=row_sum[:, tiles], in_=half_sum[:, tiles, :], axis=AXIS.X, op=ALU.add
             )
+
+        def invert_sums(half):
+            tiles = slice(half * 4, (half + 1) * 4)
             nc.vector.reciprocal(out=row_inv[:, tiles], in_=row_sum[:, tiles])
 
-        def spread_inverse(half, r):
+        def spread_inverse(half, r, banks=aux_ps):
             if r == 0:
-                inv_t[half] = aux_ps.tile([P, 4, P], F32, name="inv_t", tag="bank")
+                inv_t[half] = banks.tile([P, 4, P], F32, name="inv_t", tag="bank")
             i = half * 4 + r
             nc.tensor.transpose(
                 inv_t[half][:, r, :], row_inv[:, i : i + 1].to_broadcast([P, P]), ident_f32[:]
@@ -208,8 +207,8 @@ def tile_objectattention_pa_kernel(
                 in_=inv_t[half][:].rearrange("p r n -> p (r n)"),
             )
 
-        def attend(i):
-            ctx_ps[i] = aux_ps.tile([P, PACK, P], F32, name="ctx_ps", tag="bank")
+        def attend(i, banks=aux_ps):
+            ctx_ps[i] = banks.tile([P, PACK, P], F32, name="ctx_ps", tag="bank")
             for t in range(PACK):
                 for g in range(K_PASSES):
                     nc.tensor.matmul_mx(
@@ -240,11 +239,11 @@ def tile_objectattention_pa_kernel(
                 in_=ctx_grouped[i][:].rearrange("p n t -> p (n t)"),
             )
 
-        def project(group):
-            queries = slice(group * GROUP_COLS, (group + 1) * GROUP_COLS)
-            y_sb = y_pool.tile([P, C_CHUNKS, GROUP_COLS], F32, name="y_sb", tag="y_sb")
+        def project(first, count):
+            queries = slice(first * P, (first + count) * P)
             for pair in range(C_CHUNKS // 2):
-                y_bank = acc_ps.tile([P, 2, GROUP_COLS], F32, name="y_bank", tag="bank")
+                y_bank = acc_ps.tile([P, 2, count * P], F32, name="y_bank", tag="bank")
+                y_ps[(first, pair)] = y_bank
                 for second in range(2):
                     j = 2 * pair + second
                     nc.tensor.matmul_mx(
@@ -256,61 +255,36 @@ def tile_objectattention_pa_kernel(
                         start=True,
                         stop=True,
                     )
-                for second in range(2):
-                    j = 2 * pair + second
+
+        y_ps = {}
+
+        def finish(first, count, pair, on_vector=False, joint=False):
+            queries = slice(first * P, (first + count) * P)
+            y_sb = y_pool.tile([P, 2, count * P], F32, name="y_sb", tag="y%d" % count)
+            for second in range(2):
+                j = 2 * pair + second
+                if on_vector:
+                    nc.vector.tensor_scalar(
+                        out=y_sb[:, second, :], in0=y_ps[(first, pair)][:, second, :],
+                        scalar1=bn_scale[:, j : j + 1], scalar2=bn_bias[:, j : j + 1],
+                        op0=ALU.mult, op1=ALU.add,
+                    )
+                else:
                     nc.scalar.activation(
-                        out=y_sb[:, j, :],
-                        in_=y_bank[:, second, :],
+                        out=y_sb[:, second, :],
+                        in_=y_ps[(first, pair)][:, second, :],
                         func=ACT.Relu,
                         bias=bn_bias[:, j : j + 1],
                         scale=bn_scale[:, j : j + 1],
                     )
-                    nc.sync.dma_start(out=out_view[:, j, queries], in_=y_sb[:, j, :])
+                    if not joint:
+                        nc.sync.dma_start(out=out_view[:, j, queries], in_=y_sb[:, second, :])
+            if on_vector:
+                nc.vector.tensor_scalar_max(out=y_sb[:], in0=y_sb[:], scalar1=0.0)
+            if joint or on_vector:
+                nc.sync.dma_start(out=out_view[:, 2 * pair : 2 * pair + 2, queries], in_=y_sb[:])
 
-        for i in range(N_TILES):
-            for h in range(2):
-                s_bank[(i, h)] = acc_ps.tile([P, HALF], F32, name="s_bank", tag="bank")
-                for j in range(C_CHUNKS):
-                    nc.tensor.matmul(
-                        out=s_bank[(i, h)][:],
-                        lhsT=q_sb[:, j, i * P : (i + 1) * P],
-                        rhs=k_sb[:, j, h * HALF : (h + 1) * HALF],
-                        start=(j == 0),
-                        stop=(j == C_CHUNKS - 1),
-                    )
-                    if h == 1 and i >= E_LAG:
-                        transpose_e(i - E_LAG, j, aux_ps)
-                    if h == 0 and V_STEP <= i < V_STEP + 4:
-                        transpose_v(i - V_STEP, j)
-                    if h == 0 and i == RB_STEP:
-                        spread_inverse(0, j)
-                    if h == 0 and i == BN_STEP and j == 0:
-                        bn_t = aux_ps.tile([P, P], BF16, name="bn_t", tag="bank")
-                        nc.tensor.transpose(bn_t[:], bn_rows[:], ident_bf16[:])
-
-            nc.vector.tensor_reduce(
-                out=half_max[:, i : i + 1], in_=s_bank[(i, 0)][:], axis=AXIS.X, op=ALU.max,
-                negate=True,
-            )
-            if i == BN_STEP:
-                nc.vector.tensor_copy(out=bn_cols[:], in_=bn_t[:, 0 : 4 * C_CHUNKS])
-                gamma_c = bn_cols[:, 0:C_CHUNKS]
-                beta_c = bn_cols[:, C_CHUNKS : 2 * C_CHUNKS]
-                mean_c = bn_cols[:, 2 * C_CHUNKS : 3 * C_CHUNKS]
-                var_c = bn_cols[:, 3 * C_CHUNKS : 4 * C_CHUNKS]
-                nc.gpsimd.tensor_scalar_add(out=bn_var_eps[:], in0=var_c, scalar1=EPS)
-                nc.gpsimd.tensor_tensor(
-                    out=bn_rstd[:], in0=bn_var_eps[:], in1=minus_half[:], op=ALU.pow
-                )
-                nc.gpsimd.tensor_tensor(out=bn_scale[:], in0=gamma_c, in1=bn_rstd[:], op=ALU.mult)
-                nc.gpsimd.tensor_tensor(out=bn_shift[:], in0=mean_c, in1=bn_scale[:], op=ALU.mult)
-                nc.gpsimd.tensor_tensor(
-                    out=bn_bias[:], in0=beta_c, in1=bn_shift[:], op=ALU.subtract
-                )
-            if V_STEP <= i < V_STEP + 4:
-                evacuate_v(i - V_STEP)
-            if i == V_STEP + 2 or i == V_STEP + 4:
-                quantise_v((i - V_STEP - 2) // 2)
+        def maximum(i):
             negated = ring.tile([P, HALF], BF16, name="negated", tag="negated")
             nc.vector.tensor_scalar(
                 out=negated[:],
@@ -322,10 +296,7 @@ def tile_objectattention_pa_kernel(
                 accum_out=neg_max[:, i : i + 1],
             )
 
-            if i == RB_STEP:
-                evacuate_inverse(0)
-            if i >= E_LAG:
-                evacuate_e(i - E_LAG)
+        def exponentials(i):
             e_sb[i] = ring.tile([P, PIXELS], BF16, name="e_sb", tag="e_sb")
             for h in range(2):
                 nc.scalar.activation(
@@ -337,33 +308,156 @@ def tile_objectattention_pa_kernel(
                     accum_out=half_sum[:, i, h : h + 1],
                 )
 
-            if i >= E_LAG:
-                quantise_e(i - E_LAG)
-            if i == RB_STEP - 2:
-                invert_row_sums(0)
+        def batch_norm_vectors(bn_t):
+            nc.vector.tensor_copy(out=bn_cols[:], in_=bn_t[:, 0 : 4 * C_CHUNKS])
+            gamma_c = bn_cols[:, 0:C_CHUNKS]
+            beta_c = bn_cols[:, C_CHUNKS : 2 * C_CHUNKS]
+            mean_c = bn_cols[:, 2 * C_CHUNKS : 3 * C_CHUNKS]
+            var_c = bn_cols[:, 3 * C_CHUNKS : 4 * C_CHUNKS]
+            nc.gpsimd.tensor_scalar_add(out=bn_var_eps[:], in0=var_c, scalar1=EPS)
+            nc.gpsimd.tensor_tensor(
+                out=bn_rstd[:], in0=bn_var_eps[:], in1=minus_half[:], op=ALU.pow
+            )
+            nc.gpsimd.tensor_tensor(out=bn_scale[:], in0=gamma_c, in1=bn_rstd[:], op=ALU.mult)
+            nc.gpsimd.tensor_tensor(out=bn_shift[:], in0=mean_c, in1=bn_scale[:], op=ALU.mult)
+            nc.gpsimd.tensor_tensor(out=bn_bias[:], in0=beta_c, in1=bn_shift[:], op=ALU.subtract)
 
-        for c in range(2 * K_PASSES):
-            transpose_e(N_TILES - 2, c, acc_ps)
-        evacuate_e(N_TILES - 2)
-        for i in range(N_TILES + W_LAG - 1):
-            if i == LAST_E_ROUND:
-                for c in range(2 * K_PASSES):
-                    transpose_e(N_TILES - 1, c, acc_ps)
-                for r in range(4):
-                    spread_inverse(1, r)
-                evacuate_e(N_TILES - 1)
-                evacuate_inverse(1)
-            if i < N_TILES:
-                attend(i)
-                normalise(i)
-            if i == LAST_E_ROUND - 2:
-                invert_row_sums(1)
-            if i == LAST_E_ROUND - 1:
-                quantise_e(N_TILES - 2)
-            if i == LAST_E_ROUND:
-                quantise_e(N_TILES - 1)
-            if 1 <= i <= N_TILES:
-                quantise_ctx(i - 1)
-            group, odd = divmod(i - W_LAG, GROUP)
-            if odd == 0 and 0 <= group < N_GROUPS:
-                project(group)
+        def scores(i, h, extra=None):
+            s_bank[(i, h)] = acc_ps.tile([P, HALF], F32, name="s_bank", tag="bank")
+            for j in range(C_CHUNKS):
+                nc.tensor.matmul(
+                    out=s_bank[(i, h)][:],
+                    lhsT=q_sb[:, j, i * P : (i + 1) * P],
+                    rhs=k_sb[:, j, h * HALF : (h + 1) * HALF],
+                    start=(j == 0),
+                    stop=(j == C_CHUNKS - 1),
+                )
+                if extra is not None:
+                    extra(j)
+
+        def first_maximum(i):
+            nc.vector.tensor_reduce(
+                out=half_max[:, i : i + 1], in_=s_bank[(i, 0)][:], axis=AXIS.X, op=ALU.max,
+                negate=True,
+            )
+
+        def bn_transpose(j):
+            if j == 0:
+                bn_t[0] = aux_ps.tile([P, P], BF16, name="bn_t", tag="bank")
+                nc.tensor.transpose(bn_t[0][:], bn_rows[:], ident_bf16[:])
+
+        bn_t = {}
+        scores(0, 0)
+        first_maximum(0)
+        scores(0, 1)
+        maximum(0)
+        exponentials(0)
+        scores(1, 0)
+        first_maximum(1)
+        scores(1, 1)
+        maximum(1)
+        exponentials(1)
+        scores(2, 0, lambda j: (transpose_v(0, j),))
+        first_maximum(2)
+        evacuate_v(0, nc.vector.tensor_copy)
+        scores(2, 1, lambda j: (transpose_e(0, j, aux_ps), transpose_v(1, j),))
+        maximum(2)
+        evacuate_v(1, nc.vector.tensor_copy)
+        evacuate_e(0, nc.scalar.copy)
+        exponentials(2)
+        scores(3, 0, lambda j: (transpose_v(2, j),))
+        first_maximum(3)
+        evacuate_v(2, nc.vector.tensor_copy)
+        scores(3, 1, lambda j: (transpose_e(1, j, aux_ps), transpose_v(3, j),))
+        maximum(3)
+        evacuate_v(3, nc.scalar.copy)
+        evacuate_e(1, nc.scalar.copy)
+        exponentials(3)
+        quantise_e(0)
+        scores(4, 0)
+        first_maximum(4)
+        quantise_v(0)
+        scores(4, 1, lambda j: (transpose_e(2, j, aux_ps),))
+        maximum(4)
+        evacuate_e(2, nc.scalar.copy)
+        exponentials(4)
+        sum_rows(0)
+        quantise_e(1)
+        invert_sums(0)
+        scores(5, 0)
+        first_maximum(5)
+        quantise_v(1)
+        scores(5, 1, lambda j: (transpose_e(3, j, aux_ps),))
+        maximum(5)
+        evacuate_e(3, nc.scalar.copy)
+        exponentials(5)
+        quantise_e(2)
+        scores(6, 0, lambda j: (spread_inverse(0, j),))
+        first_maximum(6)
+        scores(6, 1, lambda j: (transpose_e(4, j, aux_ps),))
+        maximum(6)
+        evacuate_inverse(0)
+        evacuate_e(4, nc.scalar.copy)
+        exponentials(6)
+        quantise_e(3)
+        scores(7, 0, lambda j: (bn_transpose(j),))
+        first_maximum(7)
+        batch_norm_vectors(bn_t[0])
+        quantise_e(4)
+        scores(7, 1, lambda j: (transpose_e(5, j, aux_ps),))
+        maximum(7)
+        evacuate_e(5, nc.scalar.copy)
+        exponentials(7)
+        attend(0, aux_ps)
+        normalise(0)
+        attend(1, aux_ps)
+        normalise(1)
+        for c in range(4):
+            transpose_e(6, c, acc_ps)
+        evacuate_e(6, nc.scalar.copy)
+        quantise_ctx(0)
+        sum_rows(1)
+        quantise_ctx(1)
+        invert_sums(1)
+        attend(2, aux_ps)
+        normalise(2)
+        attend(3, aux_ps)
+        normalise(3)
+        quantise_e(5)
+        for c in range(4):
+            transpose_e(7, c, acc_ps)
+        for c in range(4):
+            spread_inverse(1, c, acc_ps)
+        evacuate_e(7, nc.scalar.copy)
+        evacuate_inverse(1)
+        project(0, 2)
+        finish(0, 2, 0, False, False)
+        finish(0, 2, 1, False, False)
+        attend(4, aux_ps)
+        quantise_ctx(2)
+        quantise_ctx(3)
+        quantise_e(6)
+        attend(5, aux_ps)
+        quantise_e(7)
+        normalise(4)
+        project(2, 2)
+        finish(2, 2, 0, False, False)
+        finish(2, 2, 1, False, False)
+        normalise(5)
+        attend(6, aux_ps)
+        quantise_ctx(4)
+        attend(7, aux_ps)
+        quantise_ctx(5)
+        normalise(6)
+        project(4, 2)
+        finish(4, 2, 0, False, False)
+        finish(4, 2, 1, False, False)
+        normalise(7)
+        quantise_ctx(6)
+        project(6, 1)
+        finish(6, 1, 0, False, True)
+        finish(6, 1, 1, False, True)
+        quantise_ctx(7)
+        project(7, 1)
+        finish(7, 1, 0, False, True)
+        finish(7, 1, 1, True, False)

@@ -44,8 +44,8 @@ def tile_objectattention_pa_kernel(
         keep = ctx.enter_context(tc.tile_pool(name="keep", bufs=1))
         ring = ctx.enter_context(tc.tile_pool(name="ring", bufs=3))
         y_pool = ctx.enter_context(tc.tile_pool(name="y_pool", bufs=8))
-        acc_ps = ctx.enter_context(tc.psum_pool(name="acc_ps", bufs=4))
-        aux_ps = ctx.enter_context(tc.psum_pool(name="aux_ps", bufs=4))
+        acc_ps = ctx.enter_context(tc.psum_pool(name="acc_ps", bufs=5))
+        aux_ps = ctx.enter_context(tc.psum_pool(name="aux_ps", bufs=3))
         ctx.enter_context(tc.manual_schedule())
 
         q_sb = keep.tile([P, C_CHUNKS, PIXELS], BF16)
@@ -347,13 +347,26 @@ def tile_objectattention_pa_kernel(
                 nc.tensor.transpose(bn_t[0][:], bn_rows[:], ident_bf16[:])
 
         bn_t = {}
-        scores(0, 0)
+
+        def first_scores():
+            for i in range(2):
+                s_bank[(i, 0)] = acc_ps.tile([P, HALF], F32, name="s_bank", tag="bank")
+            for j in range(C_CHUNKS):
+                for i in range(2):
+                    nc.tensor.matmul(
+                        out=s_bank[(i, 0)][:],
+                        lhsT=q_sb[:, j, i * P : (i + 1) * P],
+                        rhs=k_sb[:, j, 0:HALF],
+                        start=(j == 0),
+                        stop=(j == C_CHUNKS - 1),
+                    )
+
+        first_scores()
         first_maximum(0)
+        first_maximum(1)
         scores(0, 1)
         maximum(0)
         exponentials(0)
-        scores(1, 0)
-        first_maximum(1)
         scores(1, 1)
         maximum(1)
         exponentials(1)

@@ -26,6 +26,7 @@ GROUP = 2
 GROUP_COLS = GROUP * P
 N_GROUPS = N_TILES // GROUP
 WARM_PASSES = 3
+BATCHES = ((0, 4), (4, 4))
 
 
 FLOPS = 2 * PIXELS * PIXELS * CHANNELS * 2 + 2 * CHANNELS * CHANNELS * PIXELS
@@ -183,28 +184,33 @@ def tile_objectattention_pa_kernel(
                 in_=v_grouped[:, g].rearrange("p c t -> p (c t)"),
             )
 
-        def sum_rows(half):
-            tiles = slice(half * 4, (half + 1) * 4)
+        def sum_rows(batch):
+            first, count = BATCHES[batch]
+            tiles = slice(first, first + count)
             nc.vector.tensor_reduce(
                 out=row_sum[:, tiles], in_=half_sum[:, tiles, :], axis=AXIS.X, op=ALU.add
             )
 
-        def invert_sums(half):
-            tiles = slice(half * 4, (half + 1) * 4)
+        def invert_sums(batch):
+            first, count = BATCHES[batch]
+            tiles = slice(first, first + count)
             nc.vector.reciprocal(out=row_inv[:, tiles], in_=row_sum[:, tiles])
 
-        def spread_inverse(half, r, banks=aux_ps):
+        def spread_inverse(batch, r, banks=aux_ps):
+            first, count = BATCHES[batch]
             if r == 0:
-                inv_t[half] = banks.tile([P, 4, P], F32, name="inv_t", tag="bank")
-            i = half * 4 + r
-            nc.tensor.transpose(
-                inv_t[half][:, r, :], row_inv[:, i : i + 1].to_broadcast([P, P]), ident_f32[:]
-            )
+                inv_t[batch] = banks.tile([P, count, P], F32, name="inv_t", tag="bank")
+            if r < count:
+                i = first + r
+                nc.tensor.transpose(
+                    inv_t[batch][:, r, :], row_inv[:, i : i + 1].to_broadcast([P, P]), ident_f32[:]
+                )
 
-        def evacuate_inverse(half):
+        def evacuate_inverse(batch):
+            first, count = BATCHES[batch]
             nc.scalar.copy(
-                out=inv_spread[:, half * HALF : (half + 1) * HALF],
-                in_=inv_t[half][:].rearrange("p r n -> p (r n)"),
+                out=inv_spread[:, first * P : (first + count) * P],
+                in_=inv_t[batch][:].rearrange("p r n -> p (r n)"),
             )
 
         def attend(i, banks=aux_ps):
@@ -239,15 +245,14 @@ def tile_objectattention_pa_kernel(
                 in_=ctx_grouped[i][:].rearrange("p n t -> p (n t)"),
             )
 
-        def project(first, count):
+        def project(first, count, groups):
             queries = slice(first * P, (first + count) * P)
-            for pair in range(C_CHUNKS // 2):
-                y_bank = acc_ps.tile([P, 2, count * P], F32, name="y_bank", tag="bank")
-                y_ps[(first, pair)] = y_bank
-                for second in range(2):
-                    j = 2 * pair + second
+            for group in groups:
+                y_bank = acc_ps.tile([P, len(group), count * P], F32, name="y_bank", tag="bank")
+                for place, j in enumerate(group):
+                    y_ps[(first, j)] = y_bank[:, place, :]
                     nc.tensor.matmul_mx(
-                        out=y_bank[:, second, :],
+                        out=y_bank[:, place, :],
                         lhsT=w_codes[:, j * P : (j + 1) * P].bitcast(FP8X4),
                         lhsT_scale=w_plane[:, j * P : (j + 1) * P],
                         rhs=c_codes[:, queries].bitcast(FP8X4),
@@ -258,31 +263,34 @@ def tile_objectattention_pa_kernel(
 
         y_ps = {}
 
-        def finish(first, count, pair, on_vector=False, joint=False):
+        def finish(first, count, group, on_vector=False, joint=False):
             queries = slice(first * P, (first + count) * P)
-            y_sb = y_pool.tile([P, 2, count * P], F32, name="y_sb", tag="y%d" % count)
-            for second in range(2):
-                j = 2 * pair + second
+            y_sb = y_pool.tile(
+                [P, len(group), count * P], F32, name="y_sb", tag="y%d" % (len(group) * count)
+            )
+            for place, j in enumerate(group):
                 if on_vector:
                     nc.vector.tensor_scalar(
-                        out=y_sb[:, second, :], in0=y_ps[(first, pair)][:, second, :],
+                        out=y_sb[:, place, :], in0=y_ps[(first, j)],
                         scalar1=bn_scale[:, j : j + 1], scalar2=bn_bias[:, j : j + 1],
                         op0=ALU.mult, op1=ALU.add,
                     )
                 else:
                     nc.scalar.activation(
-                        out=y_sb[:, second, :],
-                        in_=y_ps[(first, pair)][:, second, :],
-                        func=ACT.Relu,
-                        bias=bn_bias[:, j : j + 1],
-                        scale=bn_scale[:, j : j + 1],
+                        out=y_sb[:, place, :], in_=y_ps[(first, j)], func=ACT.Relu,
+                        bias=bn_bias[:, j : j + 1], scale=bn_scale[:, j : j + 1],
                     )
                     if not joint:
-                        nc.sync.dma_start(out=out_view[:, j, queries], in_=y_sb[:, second, :])
+                        nc.sync.dma_start(out=out_view[:, j, queries], in_=y_sb[:, place, :])
             if on_vector:
-                nc.vector.tensor_scalar_max(out=y_sb[:], in0=y_sb[:], scalar1=0.0)
+                for place, j in enumerate(group):
+                    nc.vector.tensor_scalar_max(
+                        out=y_sb[:, place, :], in0=y_sb[:, place, :], scalar1=0.0
+                    )
             if joint or on_vector:
-                nc.sync.dma_start(out=out_view[:, 2 * pair : 2 * pair + 2, queries], in_=y_sb[:])
+                nc.sync.dma_start(
+                    out=out_view[:, group[0] : group[-1] + 1, queries], in_=y_sb[:]
+                )
 
         def maximum(i):
             negated = ring.tile([P, HALF], BF16, name="negated", tag="negated")
@@ -322,8 +330,8 @@ def tile_objectattention_pa_kernel(
             nc.gpsimd.tensor_tensor(out=bn_shift[:], in0=mean_c, in1=bn_scale[:], op=ALU.mult)
             nc.gpsimd.tensor_tensor(out=bn_bias[:], in0=beta_c, in1=bn_shift[:], op=ALU.subtract)
 
-        def scores(i, h, extra=None):
-            s_bank[(i, h)] = acc_ps.tile([P, HALF], F32, name="s_bank", tag="bank")
+        def scores(i, h, extra=None, banks=acc_ps):
+            s_bank[(i, h)] = banks.tile([P, HALF], F32, name="s_bank", tag="bank")
             for j in range(C_CHUNKS):
                 nc.tensor.matmul(
                     out=s_bank[(i, h)][:],
@@ -361,6 +369,26 @@ def tile_objectattention_pa_kernel(
                         stop=(j == C_CHUNKS - 1),
                     )
 
+
+        def score_pass(i, h, j):
+            if j == 0:
+                s_bank[(i, h)] = acc_ps.tile([P, HALF], F32, name="s_bank", tag="bank")
+            nc.tensor.matmul(
+                out=s_bank[(i, h)][:],
+                lhsT=q_sb[:, j, i * P : (i + 1) * P],
+                rhs=k_sb[:, j, h * HALF : (h + 1) * HALF],
+                start=(j == 0),
+                stop=(j == C_CHUNKS - 1),
+            )
+
+        def first_scores_all():
+            for i, j in ((0, 0), (0, 1), (0, 2), (1, 0), (0, 3)):
+                for h in range(2):
+                    score_pass(i, h, j)
+            for h in range(2):
+                for j in range(1, C_CHUNKS):
+                    score_pass(1, h, j)
+
         first_scores()
         first_maximum(0)
         first_maximum(1)
@@ -371,21 +399,21 @@ def tile_objectattention_pa_kernel(
         maximum(1)
         exponentials(1)
         scores(2, 0, lambda j: (transpose_v(0, j),))
-        first_maximum(2)
         evacuate_v(0, nc.vector.tensor_copy)
+        first_maximum(2)
         scores(2, 1, lambda j: (transpose_e(0, j, aux_ps), transpose_v(1, j),))
-        maximum(2)
         evacuate_v(1, nc.vector.tensor_copy)
+        maximum(2)
         evacuate_e(0, nc.scalar.copy)
-        exponentials(2)
         scores(3, 0, lambda j: (transpose_v(2, j),))
+        evacuate_v(2, nc.scalar.copy)
+        exponentials(2)
         first_maximum(3)
-        evacuate_v(2, nc.vector.tensor_copy)
         scores(3, 1, lambda j: (transpose_e(1, j, aux_ps), transpose_v(3, j),))
         maximum(3)
-        evacuate_v(3, nc.scalar.copy)
         evacuate_e(1, nc.scalar.copy)
         exponentials(3)
+        evacuate_v(3, nc.scalar.copy)
         quantise_e(0)
         scores(4, 0)
         first_maximum(4)
@@ -428,6 +456,7 @@ def tile_objectattention_pa_kernel(
         for c in range(4):
             transpose_e(6, c, acc_ps)
         evacuate_e(6, nc.scalar.copy)
+        quantise_e(5)
         quantise_ctx(0)
         sum_rows(1)
         quantise_ctx(1)
@@ -436,41 +465,40 @@ def tile_objectattention_pa_kernel(
         normalise(2)
         attend(3, aux_ps)
         normalise(3)
-        quantise_e(5)
         for c in range(4):
             transpose_e(7, c, acc_ps)
         for c in range(4):
             spread_inverse(1, c, acc_ps)
         evacuate_e(7, nc.scalar.copy)
         evacuate_inverse(1)
-        project(0, 2)
-        finish(0, 2, 0, False, False)
-        finish(0, 2, 1, False, False)
-        attend(4, aux_ps)
+        project(0, 2, ((0, 1), (2, 3)))
+        finish(0, 2, (0, 1), False, False)
+        finish(0, 2, (2, 3), False, False)
+        quantise_e(6)
         quantise_ctx(2)
         quantise_ctx(3)
-        quantise_e(6)
-        attend(5, aux_ps)
         quantise_e(7)
+        attend(4, aux_ps)
         normalise(4)
-        project(2, 2)
-        finish(2, 2, 0, False, False)
-        finish(2, 2, 1, False, False)
+        attend(5, aux_ps)
         normalise(5)
-        attend(6, aux_ps)
+        project(2, 2, ((0, 1), (2, 3)))
+        finish(2, 2, (0, 1), False, False)
+        finish(2, 2, (2, 3), False, False)
         quantise_ctx(4)
-        attend(7, aux_ps)
+        attend(6, aux_ps)
         quantise_ctx(5)
         normalise(6)
-        project(4, 2)
-        finish(4, 2, 0, False, False)
-        finish(4, 2, 1, False, False)
-        normalise(7)
+        attend(7, aux_ps)
+        project(4, 2, ((0, 1), (2, 3)))
+        finish(4, 2, (0, 1), False, False)
+        finish(4, 2, (2, 3), False, False)
         quantise_ctx(6)
-        project(6, 1)
-        finish(6, 1, 0, False, True)
-        finish(6, 1, 1, False, True)
+        normalise(7)
+        project(6, 1, ((0, 1), (2, 3)))
+        finish(6, 1, (0, 1), False, True)
+        finish(6, 1, (2, 3), False, True)
         quantise_ctx(7)
-        project(7, 1)
-        finish(7, 1, 0, False, True)
-        finish(7, 1, 1, True, False)
+        project(7, 1, ((0, 1), (2, 3)))
+        finish(7, 1, (0, 1), False, True)
+        finish(7, 1, (2, 3), True, False)

@@ -287,7 +287,9 @@ def tile_objectattention_pa_kernel(
                     nc.vector.tensor_scalar_max(
                         out=y_sb[:, place, :], in0=y_sb[:, place, :], scalar1=0.0
                     )
-            if joint or on_vector:
+                    if not joint:
+                        nc.sync.dma_start(out=out_view[:, j, queries], in_=y_sb[:, place, :])
+            if joint:
                 nc.sync.dma_start(
                     out=out_view[:, group[0] : group[-1] + 1, queries], in_=y_sb[:]
                 )
@@ -493,12 +495,9 @@ def tile_objectattention_pa_kernel(
         project(4, 2, ((0, 1), (2, 3)))
         finish(4, 2, (0, 1), False, False)
         finish(4, 2, (2, 3), False, False)
-        quantise_ctx(6)
         normalise(7)
-        project(6, 1, ((0, 1), (2, 3)))
-        finish(6, 1, (0, 1), False, True)
-        finish(6, 1, (2, 3), False, True)
+        quantise_ctx(6)
         quantise_ctx(7)
-        project(7, 1, ((0, 1), (2, 3)))
-        finish(7, 1, (0, 1), False, True)
-        finish(7, 1, (2, 3), True, False)
+        project(6, 2, ((0, 1), (2, 3)))
+        finish(6, 2, (0, 1), False, False)
+        finish(6, 2, (2, 3), True, False)

from contextlib import ExitStack

import concourse.mybir as mybir
from concourse.masks import make_identity

F32 = mybir.dt.float32
BF16 = mybir.dt.bfloat16
I32 = mybir.dt.int32
U32 = mybir.dt.uint32
U8 = mybir.dt.uint8
FP8X4 = mybir.dt.float8_e4m3fn_x4
ACT = mybir.ActivationFunctionType
ALU = mybir.AluOpType
AXIS = mybir.AxisListType

P = 128
PACK = 4
CHANNELS = 512
PIXELS = 1024
EPS = 1e-5
C_CHUNKS = CHANNELS // P
HALF = 512
N_TILES = PIXELS // P
K_PASSES = PIXELS // (P * PACK)
GROUP = 2
GROUP_COLS = GROUP * P
N_GROUPS = N_TILES // GROUP
WARM_PASSES = 3
BATCHES = ((0, 4), (4, 4))


FLOPS = 2 * PIXELS * PIXELS * CHANNELS * 2 + 2 * CHANNELS * CHANNELS * PIXELS


def tile_objectattention_pa_kernel(
    tc, q, k, v, w_up_words, w_up_scales, gamma, beta, mean, var, out
):
    nc = tc.nc
    q_view = q[0].rearrange("(j p) h w -> p j (h w)", p=P)
    k_view = k[0].rearrange("(j p) h w -> p j (h w)", p=P)
    v_view = v[0].rearrange("(p t) h w -> p t (h w)", t=PACK)
    out_view = out[0].rearrange("(j p) h w -> p j (h w)", p=P)

    with ExitStack() as ctx:
        keep = ctx.enter_context(tc.tile_pool(name="keep", bufs=1))
        ring = ctx.enter_context(tc.tile_pool(name="ring", bufs=3))
        y_pool = ctx.enter_context(tc.tile_pool(name="y_pool", bufs=8))
        acc_ps = ctx.enter_context(tc.psum_pool(name="acc_ps", bufs=5))
        aux_ps = ctx.enter_context(tc.psum_pool(name="aux_ps", bufs=3))
        ctx.enter_context(tc.manual_schedule())

        q_sb = keep.tile([P, C_CHUNKS, PIXELS], BF16)
        k_sb = keep.tile([P, C_CHUNKS, PIXELS], BF16)
        v_sb = keep.tile([P, PACK, PIXELS], BF16)
        ident_f32 = keep.tile([P, P], F32)
        ident_bf16 = keep.tile([P, P], BF16)
        bn_rows = keep.tile([P, P], BF16)
        bn_cols = keep.tile([P, 4 * C_CHUNKS], F32)
        minus_half = keep.tile([P, C_CHUNKS], F32)
        bn_var_eps = keep.tile([P, C_CHUNKS], F32)
        bn_rstd = keep.tile([P, C_CHUNKS], F32)
        bn_scale = keep.tile([P, C_CHUNKS], F32)
        bn_shift = keep.tile([P, C_CHUNKS], F32)
        bn_bias = keep.tile([P, C_CHUNKS], F32)
        warm_in = keep.tile([P, HALF], BF16)
        table_in = keep.tile([P, 1], F32)
        table_out = keep.tile([P, 1], F32)
        half_max = keep.tile([P, N_TILES], F32)
        neg_max = keep.tile([P, N_TILES], F32)
        half_sum = keep.tile([P, N_TILES, 2], F32)
        row_sum = keep.tile([P, N_TILES], F32)
        row_inv = keep.tile([P, N_TILES], F32)
        inv_spread = keep.tile([P, PIXELS], F32)
        w_codes = keep.tile([P, CHANNELS], U32, align_bytes=64)
        w_plane = keep.tile([P, CHANNELS], U8, align_bytes=64)
        v_grouped = keep.tile([P, K_PASSES, CHANNELS, PACK], BF16, align_bytes=64)
        v_codes = keep.tile([P, K_PASSES, CHANNELS], U32, align_bytes=64)
        v_plane = keep.tile([P, K_PASSES, CHANNELS], U8, align_bytes=64)
        e_codes = keep.tile([P, N_TILES, K_PASSES, P], U32, align_bytes=64)
        e_plane = keep.tile([P, N_TILES, K_PASSES, P], U8, align_bytes=64)
        c_codes = keep.tile([P, PIXELS], U32, align_bytes=64)
        c_plane = keep.tile([P, PIXELS], U8, align_bytes=64)

        nc.vector.memset(warm_in[:].bitcast(I32), 0)
        nc.vector.memset(table_in[:], 0.0)
        nc.vector.memset(bn_rows[:], 0.0)
        nc.vector.memset(w_plane[:].bitcast(I32), 0)
        nc.scalar.activation(out=table_out[:], in_=table_in[:], func=ACT.Exp)
        make_identity(nc, ident_bf16[:])
        make_identity(nc, ident_f32[:])
        nc.gpsimd.memset(minus_half[:], -0.5)

        warm_ps = aux_ps.tile([P, HALF], F32, name="warm_ps", tag="bank")
        for warm in range(WARM_PASSES):
            nc.tensor.matmul(
                out=warm_ps[:], lhsT=warm_in[:, 0:P], rhs=warm_in[:], start=True, stop=True
            )

        first_q = GROUP_COLS
        for j in range(C_CHUNKS):
            nc.sync.dma_start(out=q_sb[:, j, 0:first_q], in_=q_view[:, j, 0:first_q])
            nc.sync.dma_start(out=k_sb[:, j, 0:HALF], in_=k_view[:, j, 0:HALF])
        for pair in range(2):
            chunks = slice(2 * pair, 2 * pair + 2)
            nc.sync.dma_start(out=k_sb[:, chunks, HALF:PIXELS], in_=k_view[:, chunks, HALF:PIXELS])
        nc.sync.dma_start(out=q_sb[:, :, first_q:HALF], in_=q_view[:, :, first_q:HALF])
        for pair in range(2):
            rows = slice(2 * pair, 2 * pair + 2)
            nc.sync.dma_start(out=v_sb[:, rows, :], in_=v_view[:, rows, :])
        nc.sync.dma_start(out=q_sb[:, :, HALF:PIXELS], in_=q_view[:, :, HALF:PIXELS])
        nc.sync.dma_start(
            out=w_codes[:].bitcast(I32),
            in_=w_up_words[0].rearrange("p n t -> p (n t)").bitcast(I32),
        )
        for quad in range(4):
            nc.sync.dma_start(
                out=w_plane[32 * quad : 32 * quad + 4, :].bitcast(I32),
                in_=w_up_scales[0, 4 * quad : 4 * quad + 4, :].bitcast(I32),
            )
        for row, vector in enumerate((gamma, beta, mean, var)):
            nc.sync.dma_start(
                out=bn_rows[C_CHUNKS * row : C_CHUNKS * (row + 1), :],
                in_=vector.rearrange("(j p) -> j p", p=P),
            )

        s_bank = {}
        e_sb = {}
        e_t = {}
        e_grouped = {}
        v_t = {}
        inv_t = {}
        ctx_ps = {}
        ctx_grouped = {}
        v_words = v_sb[:].bitcast(F32)

        def transpose_e(i, c, banks):
            if c == 0:
                e_t[i] = banks.tile([P, 2 * K_PASSES, P], F32, name="e_t", tag="bank")
            nc.tensor.transpose(
                e_t[i][:, c, :], e_sb[i][:].bitcast(F32)[:, c * P : (c + 1) * P], ident_f32[:]
            )

        def evacuate_e(i, copy=nc.scalar.copy):
            e_grouped[i] = ring.tile(
                [P, K_PASSES, P, PACK], BF16, name="e_grouped", tag="e_grouped", align_bytes=64
            )
            copy(
                out=e_grouped[i][:].bitcast(F32),
                in_=e_t[i][:].rearrange("p (g u) n -> p g n u", u=2),
            )

        def quantise_e(i):
            nc.vector.quantize_mx(
                out=e_codes[:, i].rearrange("p g n -> p (g n)").bitcast(FP8X4),
                scales=e_plane[:, i].rearrange("p g n -> p (g n)"),
                in_=e_grouped[i][:].rearrange("p g n t -> p (g n t)"),
            )

        def transpose_v(bank, r):
            pair, g = divmod(bank, 2)
            u, second = divmod(r, 2)
            t = 2 * pair + second
            if r == 0:
                v_t[bank] = aux_ps.tile([P, 2, 2 * P], F32, name="v_t", tag="bank")
            first_word = (2 * g + u) * P
            nc.tensor.transpose(
                v_t[bank][:, u, second * P : (second + 1) * P],
                v_words[:, t, first_word : first_word + P],
                ident_f32[:],
            )

        def evacuate_v(bank, copy):
            pair, g = divmod(bank, 2)
            columns = slice(pair * 2 * P, (pair + 1) * 2 * P)
            copy(
                out=v_grouped[:, g, columns, :].bitcast(F32),
                in_=v_t[bank][:].rearrange("p u c -> p c u"),
            )

        def quantise_v(g):
            nc.vector.quantize_mx(
                out=v_codes[:, g, :].bitcast(FP8X4),
                scales=v_plane[:, g, :],
                in_=v_grouped[:, g].rearrange("p c t -> p (c t)"),
            )

        def sum_rows(batch):
            first, count = BATCHES[batch]
            tiles = slice(first, first + count)
            nc.vector.tensor_reduce(
                out=row_sum[:, tiles], in_=half_sum[:, tiles, :], axis=AXIS.X, op=ALU.add
            )

        def invert_sums(batch):
            first, count = BATCHES[batch]
            tiles = slice(first, first + count)
            nc.vector.reciprocal(out=row_inv[:, tiles], in_=row_sum[:, tiles])

        def spread_inverse(batch, r, banks=aux_ps):
            first, count = BATCHES[batch]
            if r == 0:
                inv_t[batch] = banks.tile([P, count, P], F32, name="inv_t", tag="bank")
            if r < count:
                i = first + r
                nc.tensor.transpose(
                    inv_t[batch][:, r, :], row_inv[:, i : i + 1].to_broadcast([P, P]), ident_f32[:]
                )

        def evacuate_inverse(batch):
            first, count = BATCHES[batch]
            nc.scalar.copy(
                out=inv_spread[:, first * P : (first + count) * P],
                in_=inv_t[batch][:].rearrange("p r n -> p (r n)"),
            )

        def attend(i, banks=aux_ps):
            ctx_ps[i] = banks.tile([P, PACK, P], F32, name="ctx_ps", tag="bank")
            for t in range(PACK):
                for g in range(K_PASSES):
                    nc.tensor.matmul_mx(
                        out=ctx_ps[i][:, t, :],
                        lhsT=v_codes[:, g, t * P : (t + 1) * P].bitcast(FP8X4),
                        lhsT_scale=v_plane[:, g, t * P : (t + 1) * P],
                        rhs=e_codes[:, i, g, :].bitcast(FP8X4),
                        rhs_scale=e_plane[:, i, g, :],
                        start=(g == 0),
                        stop=(g == K_PASSES - 1),
                    )

        def normalise(i):
            ctx_grouped[i] = ring.tile(
                [P, P, PACK], BF16, name="ctx_grouped", tag="ctx_grouped", align_bytes=64
            )
            nc.vector.tensor_tensor(
                out=ctx_grouped[i][:],
                in0=ctx_ps[i][:].rearrange("p t n -> p n t"),
                in1=inv_spread[:, i * P : (i + 1) * P].unsqueeze(2).to_broadcast([P, P, PACK]),
                op=ALU.mult,
            )

        def quantise_ctx(i):
            nc.vector.quantize_mx(
                out=c_codes[:, i * P : (i + 1) * P].bitcast(FP8X4),
                scales=c_plane[:, i * P : (i + 1) * P],
                in_=ctx_grouped[i][:].rearrange("p n t -> p (n t)"),
            )

        def project(first, count, groups):
            queries = slice(first * P, (first + count) * P)
            for group in groups:
                y_bank = acc_ps.tile([P, len(group), count * P], F32, name="y_bank", tag="bank")
                for place, j in enumerate(group):
                    y_ps[(first, j)] = y_bank[:, place, :]
                    nc.tensor.matmul_mx(
                        out=y_bank[:, place, :],
                        lhsT=w_codes[:, j * P : (j + 1) * P].bitcast(FP8X4),
                        lhsT_scale=w_plane[:, j * P : (j + 1) * P],
                        rhs=c_codes[:, queries].bitcast(FP8X4),
                        rhs_scale=c_plane[:, queries],
                        start=True,
                        stop=True,
                    )

        y_ps = {}

        def finish(first, count, group, on_vector=False, joint=False):
            queries = slice(first * P, (first + count) * P)
            y_sb = y_pool.tile(
                [P, len(group), count * P], F32, name="y_sb", tag="y%d" % (len(group) * count)
            )
            for place, j in enumerate(group):
                if on_vector:
                    nc.vector.tensor_scalar(
                        out=y_sb[:, place, :], in0=y_ps[(first, j)],
                        scalar1=bn_scale[:, j : j + 1], scalar2=bn_bias[:, j : j + 1],
                        op0=ALU.mult, op1=ALU.add,
                    )
                else:
                    nc.scalar.activation(
                        out=y_sb[:, place, :], in_=y_ps[(first, j)], func=ACT.Relu,
                        bias=bn_bias[:, j : j + 1], scale=bn_scale[:, j : j + 1],
                    )
                    if not joint:
                        nc.sync.dma_start(out=out_view[:, j, queries], in_=y_sb[:, place, :])
            if on_vector:
                for place, j in enumerate(group):
                    nc.vector.tensor_scalar_max(
                        out=y_sb[:, place, :], in0=y_sb[:, place, :], scalar1=0.0
                    )
                    if not joint:
                        nc.sync.dma_start(out=out_view[:, j, queries], in_=y_sb[:, place, :])
            if joint:
                nc.sync.dma_start(
                    out=out_view[:, group[0] : group[-1] + 1, queries], in_=y_sb[:]
                )

        def maximum(i):
            negated = ring.tile([P, HALF], BF16, name="negated", tag="negated")
            nc.vector.tensor_scalar(
                out=negated[:],
                in0=s_bank[(i, 1)][:],
                scalar1=-1.0,
                scalar2=half_max[:, i : i + 1],
                op0=ALU.mult,
                op1=ALU.min,
                accum_out=neg_max[:, i : i + 1],
            )

        def exponentials(i):
            e_sb[i] = ring.tile([P, PIXELS], BF16, name="e_sb", tag="e_sb")
            for h in range(2):
                nc.scalar.activation(
                    out=e_sb[i][:, h * HALF : (h + 1) * HALF],
                    in_=s_bank[(i, h)][:],
                    func=ACT.Exp,
                    bias=neg_max[:, i : i + 1],
                    scale=1.0,
                    accum_out=half_sum[:, i, h : h + 1],
                )

        def batch_norm_vectors(bn_t):
            nc.vector.tensor_copy(out=bn_cols[:], in_=bn_t[:, 0 : 4 * C_CHUNKS])
            gamma_c = bn_cols[:, 0:C_CHUNKS]
            beta_c = bn_cols[:, C_CHUNKS : 2 * C_CHUNKS]
            mean_c = bn_cols[:, 2 * C_CHUNKS : 3 * C_CHUNKS]
            var_c = bn_cols[:, 3 * C_CHUNKS : 4 * C_CHUNKS]
            nc.gpsimd.tensor_scalar_add(out=bn_var_eps[:], in0=var_c, scalar1=EPS)
            nc.gpsimd.tensor_tensor(
                out=bn_rstd[:], in0=bn_var_eps[:], in1=minus_half[:], op=ALU.pow
            )
            nc.gpsimd.tensor_tensor(out=bn_scale[:], in0=gamma_c, in1=bn_rstd[:], op=ALU.mult)
            nc.gpsimd.tensor_tensor(out=bn_shift[:], in0=mean_c, in1=bn_scale[:], op=ALU.mult)
            nc.gpsimd.tensor_tensor(out=bn_bias[:], in0=beta_c, in1=bn_shift[:], op=ALU.subtract)

        def scores(i, h, extra=None, banks=acc_ps):
            s_bank[(i, h)] = banks.tile([P, HALF], F32, name="s_bank", tag="bank")
            for j in range(C_CHUNKS):
                nc.tensor.matmul(
                    out=s_bank[(i, h)][:],
                    lhsT=q_sb[:, j, i * P : (i + 1) * P],
                    rhs=k_sb[:, j, h * HALF : (h + 1) * HALF],
                    start=(j == 0),
                    stop=(j == C_CHUNKS - 1),
                )
                if extra is not None:
                    extra(j)

        def first_maximum(i):
            nc.vector.tensor_reduce(
                out=half_max[:, i : i + 1], in_=s_bank[(i, 0)][:], axis=AXIS.X, op=ALU.max,
                negate=True,
            )

        def bn_transpose(j):
            if j == 0:
                bn_t[0] = aux_ps.tile([P, P], BF16, name="bn_t", tag="bank")
                nc.tensor.transpose(bn_t[0][:], bn_rows[:], ident_bf16[:])

        bn_t = {}

        def first_scores():
            for i in range(2):
                s_bank[(i, 0)] = acc_ps.tile([P, HALF], F32, name="s_bank", tag="bank")
            for j in range(C_CHUNKS):
                for i in range(2):
                    nc.tensor.matmul(
                        out=s_bank[(i, 0)][:],
                        lhsT=q_sb[:, j, i * P : (i + 1) * P],
                        rhs=k_sb[:, j, 0:HALF],
                        start=(j == 0),
                        stop=(j == C_CHUNKS - 1),
                    )


        def score_pass(i, h, j):
            if j == 0:
                s_bank[(i, h)] = acc_ps.tile([P, HALF], F32, name="s_bank", tag="bank")
            nc.tensor.matmul(
                out=s_bank[(i, h)][:],
                lhsT=q_sb[:, j, i * P : (i + 1) * P],
                rhs=k_sb[:, j, h * HALF : (h + 1) * HALF],
                start=(j == 0),
                stop=(j == C_CHUNKS - 1),
            )

        def first_scores_all():
            for i, j in ((0, 0), (0, 1), (0, 2), (1, 0), (0, 3)):
                for h in range(2):
                    score_pass(i, h, j)
            for h in range(2):
                for j in range(1, C_CHUNKS):
                    score_pass(1, h, j)

        first_scores()
        first_maximum(0)
        first_maximum(1)
        scores(0, 1)
        maximum(0)
        exponentials(0)
        scores(1, 1)
        maximum(1)
        exponentials(1)
        scores(2, 0, lambda j: (transpose_v(0, j),))
        evacuate_v(0, nc.vector.tensor_copy)
        first_maximum(2)
        scores(2, 1, lambda j: (transpose_e(0, j, aux_ps), transpose_v(1, j),))
        evacuate_v(1, nc.vector.tensor_copy)
        maximum(2)
        evacuate_e(0, nc.scalar.copy)
        scores(3, 0, lambda j: (transpose_v(2, j),))
        evacuate_v(2, nc.scalar.copy)
        exponentials(2)
        first_maximum(3)
        scores(3, 1, lambda j: (transpose_e(1, j, aux_ps), transpose_v(3, j),))
        maximum(3)
        evacuate_e(1, nc.scalar.copy)
        exponentials(3)
        evacuate_v(3, nc.scalar.copy)
        quantise_e(0)
        scores(4, 0)
        first_maximum(4)
        quantise_v(0)
        scores(4, 1, lambda j: (transpose_e(2, j, aux_ps),))
        maximum(4)
        evacuate_e(2, nc.scalar.copy)
        exponentials(4)
        sum_rows(0)
        quantise_e(1)
        invert_sums(0)
        scores(5, 0)
        first_maximum(5)
        quantise_v(1)
        scores(5, 1, lambda j: (transpose_e(3, j, aux_ps),))
        maximum(5)
        evacuate_e(3, nc.scalar.copy)
        exponentials(5)
        quantise_e(2)
        scores(6, 0, lambda j: (spread_inverse(0, j),))
        first_maximum(6)
        scores(6, 1, lambda j: (transpose_e(4, j, aux_ps),))
        maximum(6)
        evacuate_inverse(0)
        evacuate_e(4, nc.scalar.copy)
        exponentials(6)
        quantise_e(3)
        scores(7, 0, lambda j: (bn_transpose(j),))
        first_maximum(7)
        batch_norm_vectors(bn_t[0])
        quantise_e(4)
        scores(7, 1, lambda j: (transpose_e(5, j, aux_ps),))
        maximum(7)
        evacuate_e(5, nc.scalar.copy)
        exponentials(7)
        attend(0, aux_ps)
        normalise(0)
        attend(1, aux_ps)
        normalise(1)
        for c in range(4):
            transpose_e(6, c, acc_ps)
        evacuate_e(6, nc.scalar.copy)
        quantise_e(5)
        quantise_ctx(0)
        sum_rows(1)
        quantise_ctx(1)
        invert_sums(1)
        attend(2, aux_ps)
        normalise(2)
        attend(3, aux_ps)
        normalise(3)
        for c in range(4):
            transpose_e(7, c, acc_ps)
        for c in range(4):
            spread_inverse(1, c, acc_ps)
        evacuate_e(7, nc.scalar.copy)
        evacuate_inverse(1)
        project(0, 2, ((0, 1), (2, 3)))
        finish(0, 2, (0, 1), False, False)
        finish(0, 2, (2, 3), False, False)
        quantise_e(6)
        quantise_ctx(2)
        quantise_ctx(3)
        quantise_e(7)
        attend(4, aux_ps)
        normalise(4)
        attend(5, aux_ps)
        normalise(5)
        project(2, 2, ((0, 1), (2, 3)))
        finish(2, 2, (0, 1), False, False)
        finish(2, 2, (2, 3), False, False)
        quantise_ctx(4)
        attend(6, aux_ps)
        quantise_ctx(5)
        normalise(6)
        attend(7, aux_ps)
        project(4, 2, ((0, 1), (2, 3)))
        finish(4, 2, (0, 1), False, False)
        finish(4, 2, (2, 3), False, False)
        normalise(7)
        quantise_ctx(6)
        quantise_ctx(7)
        project(6, 2, ((0, 1), (2, 3)))
        finish(6, 2, (0, 1), False, False)
        finish(6, 2, (2, 3), True, False)
